import numpy as np
import ml_dtypes


def mxq(x, axis, fmt="e4m3"):
    dtype, down = {"e4m3": (ml_dtypes.float8_e4m3fn, 7), "e5m2": (ml_dtypes.float8_e5m2, 14)}[fmt]
    v = np.moveaxis(np.asarray(x, np.float32).astype(ml_dtypes.bfloat16).astype(np.float64), axis, -1)
    blocks = v.reshape(v.shape[:-1] + (-1, 32))
    amax = np.abs(blocks).max(-1, keepdims=True)
    byte = np.maximum(np.where(amax > 0, np.frexp(amax)[1] - 1 + 127, 0) - down, 1)
    scale = np.exp2(byte - 127.0)
    codes = (blocks / scale).astype(np.float32).astype(dtype).astype(np.float64)
    return np.moveaxis((codes * scale).reshape(v.shape), -1, axis)


WIDE = False


def mx_kscale(k):
    if not WIDE:
        return np.ones(k)
    levels = np.array([10, -10, 5, -5, 0])
    a = np.random.permutation(np.resize(levels, k // 512 * 4)).reshape(k // 512, 4)
    idx = np.arange(k)
    return np.exp2(a[idx // 512, idx % 128 // 32])


BF16 = ml_dtypes.bfloat16


def bf(x):
    return np.asarray(x, np.float32).astype(BF16)


def f64(x):
    return np.asarray(x).astype(np.float64)


N, V, E1, E2, C, T, EMB = 4096, 4096, 1024, 512, 128, 512, 1024
BN_EPS = 1e-5


def softplus(v):
    return np.log(1.0 + np.exp(v))


def bn(x, gamma, beta):
    m = x.mean(0)
    v = x.var(0)
    return (x - m) / np.sqrt(v + BN_EPS) * gamma + beta


def setup_inputs():
    s = mx_kscale(E1)
    return {"en1": bf(softplus(np.random.standard_normal((N, E1))) * s),
            "eps": bf(np.random.standard_normal((N, C))),
            "W2": bf(np.random.standard_normal((E2, E1)) / np.sqrt(E1) / s[None, :]),
            "b2": bf(np.random.standard_normal(E2) * 0.3),
            "Wm": bf(np.random.standard_normal((C, E2)) / np.sqrt(E2)),
            "Wv": bf(np.random.standard_normal((C, E2)) / np.sqrt(E2)),
            "gm": bf(0.5 * (1.0 + 0.1 * np.random.standard_normal(C))),
            "betam": bf(np.random.standard_normal(C) * 0.1),
            "gv": bf(0.5 * (1.0 + 0.1 * np.random.standard_normal(C))),
            "betav": bf(-1.5 + 0.1 * np.random.standard_normal(C))}


def reference(en1, eps, W2, b2, Wm, Wv, gm, betam, gv, betav):
    en2 = softplus((mxq(f64(en1), 1, "e4m3") @ mxq(f64(W2), 1, "e4m3").T) + f64(b2))
    en2q = mxq(en2, 1, "e4m3")
    posterior_mean = bn(en2q @ mxq(f64(Wm), 1, "e4m3").T, f64(gm), f64(betam))
    posterior_logvar = bn(en2q @ mxq(f64(Wv), 1, "e4m3").T, f64(gv), f64(betav))
    posterior_var = np.exp(posterior_logvar)
    return posterior_mean + np.sqrt(posterior_var) * f64(eps)

@@ -1,0 +1,315 @@
+from contextlib import ExitStack
+
+import concourse.mybir as mybir
+from concourse.masks import make_identity
+
+F32 = mybir.dt.float32
+BF16 = mybir.dt.bfloat16
+U32 = mybir.dt.uint32
+U8 = mybir.dt.uint8
+FP8X4 = mybir.dt.float8_e4m3fn_x4
+ACT = mybir.ActivationFunctionType
+ALU = mybir.AluOpType
+
+P = 128
+PACK = 4
+ROWS, K1, HIDDEN, OUTS = 4096, 1024, 512, 128
+CHUNK = 512
+CHUNKS = ROWS // CHUNK
+SUB = CHUNK // P
+PASSES = K1 // (P * PACK)
+HALF = CHUNK // 2
+BN_EPS = 1e-5
+
+FIRST_BATCH = 2
+LEAD = 2
+RAW_BUFS = 4
+
+FLOPS = 2 * ROWS * K1 * HIDDEN + 2 * 2 * ROWS * HIDDEN * OUTS
+
+
+def tile_model_pa_t_kernel(tc, en1, eps, W2, b2, Wm, Wv, gm, betam, gv, betav, out):
+    nc = tc.nc
+    en1_chunks = en1.rearrange("(g p j) k -> g p (j k)", p=P, j=SUB)
+    w2_rows = W2.rearrange("(p j) k -> p (j k)", j=SUB)
+    eps_chunks = eps.rearrange("(g p j) c -> p g (j c)", p=P, j=SUB)
+    out_chunks = out.rearrange("(g p j) c -> g p (j c)", p=P, j=SUB)
+
+    with ExitStack() as ctx:
+        ctx.enter_context(tc.manual_schedule())
+        keep = ctx.enter_context(tc.tile_pool(name="keep", bufs=1))
+        raw_pool = ctx.enter_context(tc.tile_pool(name="raw", bufs=RAW_BUFS))
+        grouped_pool = ctx.enter_context(tc.tile_pool(name="grouped", bufs=4))
+        codes_pool = ctx.enter_context(tc.tile_pool(name="codes", bufs=LEAD + 3))
+        exp_pool = ctx.enter_context(tc.tile_pool(name="exp", bufs=max(FIRST_BATCH, CHUNKS - FIRST_BATCH)))
+        en2_pool = ctx.enter_context(tc.tile_pool(name="en2", bufs=4))
+        en2_codes_pool = ctx.enter_context(tc.tile_pool(name="en2codes", bufs=CHUNKS))
+        tail_pool = ctx.enter_context(tc.tile_pool(name="tail", bufs=3))
+        psum = ctx.enter_context(tc.psum_pool(name="psum", bufs=4))
+
+        raw = {}
+        banks = {}
+        grouped = {}
+        codes = {}
+        scales = {}
+        sums = {}
+        expo = {}
+        en2 = {}
+        en2_codes = {}
+        en2_scales = {}
+        heads = {}
+
+        def load_chunk(g):
+            x_raw = raw_pool.tile([P, SUB * K1], BF16)
+            nc.sync.dma_start(out=x_raw[:], in_=en1_chunks[g])
+            raw[g] = x_raw
+
+        load_chunk(0)
+        w2_raw = keep.tile([P, SUB * K1], BF16)
+        nc.sync.dma_start(out=w2_raw[:], in_=w2_rows)
+        raw["w2"] = w2_raw
+        wm_raw = keep.tile([P, HIDDEN], BF16)
+        nc.sync.dma_start(out=wm_raw[:], in_=Wm)
+        wv_raw = keep.tile([P, HIDDEN], BF16)
+        nc.sync.dma_start(out=wv_raw[:], in_=Wv)
+        for g in range(1, RAW_BUFS):
+            load_chunk(g)
+
+        b2_raw = keep.tile([P, PACK], BF16)
+        gm_raw = keep.tile([P, 1], BF16)
+        gv_raw = keep.tile([P, 1], BF16)
+        betam_raw = keep.tile([P, 1], BF16)
+        betav_raw = keep.tile([P, 1], BF16)
+        with nc.allow_non_contiguous_dma(reason="128 short pieces, once"):
+            nc.scalar.dma_start(out=b2_raw[:], in_=b2.rearrange("(p m) -> p m", m=PACK))
+            nc.scalar.dma_start(out=gm_raw[:], in_=gm.rearrange("(p o) -> p o", o=1))
+            nc.scalar.dma_start(out=gv_raw[:], in_=gv.rearrange("(p o) -> p o", o=1))
+            nc.scalar.dma_start(out=betam_raw[:], in_=betam.rearrange("(p o) -> p o", o=1))
+            nc.scalar.dma_start(out=betav_raw[:], in_=betav.rearrange("(p o) -> p o", o=1))
+
+        one = keep.tile([P, 1], F32)
+        nc.vector.memset(one[:], 1.0)
+        warm = keep.tile([P, 1], F32)
+        nc.scalar.activation(out=warm[:], in_=one[:], func=ACT.Exp)
+
+        ident = keep.tile([P, P], F32)
+        make_identity(nc, ident[:])
+        neg_half = keep.tile([P, 2], F32)
+        nc.gpsimd.memset(neg_half[:], -0.5)
+        b2_f32 = keep.tile([P, PACK], F32)
+        nc.gpsimd.tensor_copy(out=b2_f32[:], in_=b2_raw[:])
+        gain = keep.tile([P, 2], F32)
+        shift = keep.tile([P, 2], F32)
+        nc.gpsimd.tensor_copy(out=gain[:, 0:1], in_=gm_raw[:])
+        nc.gpsimd.tensor_scalar(out=gain[:, 1:2], in0=gv_raw[:], scalar1=0.5, scalar2=0.0, op0=ALU.mult, op1=ALU.add)
+        nc.gpsimd.tensor_copy(out=shift[:, 0:1], in_=betam_raw[:])
+        nc.gpsimd.tensor_scalar(out=shift[:, 1:2], in0=betav_raw[:], scalar1=0.5, scalar2=0.0, op0=ALU.mult, op1=ALU.add)
+
+        def transpose_block(block):
+            words = raw[block][:].bitcast(F32)
+            for c in range(PASSES):
+                for h in range(2):
+                    bank = psum.tile([P, CHUNK], F32, tag="bank")
+                    for jj in range(2):
+                        for u in range(2):
+                            first = (2 * h + jj) * (K1 // 2) + 256 * c + P * u
+                            nc.tensor.transpose(
+                                bank[:, HALF * u + P * jj : HALF * u + P * (jj + 1)],
+                                words[:, first : first + P],
+                                ident[:],
+                            )
+                    banks[(block, c, h)] = bank
+
+        def open_block(block, pool):
+            for c in range(PASSES):
+                pass_in = grouped_pool.tile([P, CHUNK * PACK], BF16, align_bytes=64, tag="grouped")
+                grouped[(block, c)] = pass_in
+            block_codes = pool.tile([P, PASSES, CHUNK], U32, align_bytes=64, tag="codes")
+            block_scales = pool.tile([P, PASSES, CHUNK], U8, align_bytes=64, tag="scales")
+            codes[block] = block_codes
+            scales[block] = block_scales
+
+        def copy_out(copy, block, c, h):
+            words = grouped[(block, c)][:].bitcast(F32)
+            copy(
+                out=words[:, CHUNK * h : CHUNK * (h + 1)].rearrange("p (r u) -> p r u", u=2),
+                in_=banks[(block, c, h)][:].rearrange("p (u r) -> p r u", u=2),
+            )
+
+        def quantise(block, c):
+            nc.vector.quantize_mx(
+                out=codes[block][:, c, :].bitcast(FP8X4),
+                scales=scales[block][:, c, :],
+                in_=grouped[(block, c)][:],
+            )
+
+        def front(g, late):
+            transpose_block(g)
+            if g + RAW_BUFS < CHUNKS:
+                load_chunk(g + RAW_BUFS)
+            open_block(g, codes_pool)
+            copy_out(nc.vector.tensor_copy, g, 0, 0)
+            if late is not None:
+                quantise(late, 1)
+            copy_out(nc.vector.tensor_copy, g, 0, 1)
+            copy_out(nc.vector.tensor_copy, g, 1, 0)
+            quantise(g, 0)
+            copy_out(nc.vector.tensor_copy, g, 1, 1)
+
+        front(0, None)
+
+        transpose_block("w2")
+        open_block("w2", keep)
+        for c in range(PASSES):
+            for h in range(2):
+                copy_out(nc.scalar.copy, "w2", c, h)
+        head_bank = psum.tile([P, CHUNK], F32, tag="bank")
+        for branch, head_raw in enumerate((wm_raw, wv_raw)):
+            planes = head_raw[:].bitcast(F32).rearrange("p (q u) -> p u q", u=2)
+            for u in range(2):
+                nc.tensor.transpose(
+                    head_bank[:, HALF * u + P * branch : HALF * u + P * (branch + 1)], planes[:, u, :], ident[:]
+                )
+        head_grouped = keep.tile([P, 2 * OUTS * PACK], BF16, align_bytes=64)
+        nc.scalar.copy(
+            out=head_grouped[:].bitcast(F32).rearrange("p (r u) -> p r u", u=2),
+            in_=head_bank[:].rearrange("p (u r) -> p r u", u=2),
+        )
+        head_codes = keep.tile([P, 2 * OUTS], U32, align_bytes=64)
+        head_scales = keep.tile([P, 2 * OUTS], U8, align_bytes=64)
+        quantise("w2", 0)
+        quantise(0, 1)
+        quantise("w2", 1)
+        nc.vector.quantize_mx(out=head_codes[:].bitcast(FP8X4), scales=head_scales[:], in_=head_grouped[:])
+
+        front(1, None)
+
+        def first_product(g):
+            for m in range(PACK):
+                acc = psum.tile([P, CHUNK], F32, tag="acc")
+                for c in range(PASSES):
+                    nc.tensor.matmul_mx(
+                        out=acc[:],
+                        lhsT=codes["w2"][:, c, P * m : P * (m + 1)].bitcast(FP8X4),
+                        lhsT_scale=scales["w2"][:, c, P * m : P * (m + 1)],
+                        rhs=codes[g][:, c, :].bitcast(FP8X4),
+                        rhs_scale=scales[g][:, c, :],
+                        start=(c == 0),
+                        stop=(c == PASSES - 1),
+                    )
+                sums[(g, m)] = acc
+
+        def exponentials(g):
+            e = exp_pool.tile([P, PACK, CHUNK], F32)
+            for m in range(PACK):
+                nc.scalar.activation(out=e[:, m, :], in_=sums[(g, m)][:], func=ACT.Exp, bias=b2_f32[:, m : m + 1])
+            expo[g] = e
+
+        def logarithm(g):
+            soft = en2_pool.tile([P, CHUNK * PACK], BF16, align_bytes=64)
+            nc.scalar.activation(
+                out=soft[:].rearrange("p (q i t) -> p q t i", i=4, t=PACK),
+                in_=expo[g][:].rearrange("p t (q i) -> p q t i", i=4),
+                func=ACT.Ln,
+                bias=one[:],
+            )
+            en2[g] = soft
+
+        def quantise_en2(g):
+            soft_codes = en2_codes_pool.tile([P, CHUNK], U32, align_bytes=64)
+            soft_scales = en2_codes_pool.tile([P, CHUNK], U8, align_bytes=64)
+            nc.vector.quantize_mx(out=soft_codes[:].bitcast(FP8X4), scales=soft_scales[:], in_=en2[g][:])
+            en2_codes[g] = soft_codes
+            en2_scales[g] = soft_scales
+
+        def second_products(g, tag):
+            pair = []
+            for branch in range(2):
+                head = psum.tile([P, CHUNK], F32, tag=tag)
+                nc.tensor.matmul_mx(
+                    out=head[:],
+                    lhsT=head_codes[:, OUTS * branch : OUTS * (branch + 1)].bitcast(FP8X4),
+                    lhsT_scale=head_scales[:, OUTS * branch : OUTS * (branch + 1)],
+                    rhs=en2_codes[g][:].bitcast(FP8X4),
+                    rhs_scale=en2_scales[g][:],
+                    start=True,
+                    stop=True,
+                )
+                pair.append(head)
+            heads[g] = pair
+
+        stats = keep.tile([P, 2, CHUNKS, 6], F32)
+
+        def statistics(g):
+            for branch in range(2):
+                nc.vector.bn_stats(out=stats[:, branch, g, :], in_=heads[g][branch][:])
+
+        eps_rows = keep.tile([P, CHUNKS, CHUNK], BF16)
+        for g in range(CHUNKS):
+            if g + LEAD < CHUNKS:
+                front(g + LEAD, g + LEAD - 1)
+            elif g + LEAD == CHUNKS:
+                quantise(CHUNKS - 1, 1)
+                nc.sync.dma_start(out=eps_rows[:], in_=eps_chunks)
+            first_product(g)
+            if g == FIRST_BATCH:
+                for q in range(FIRST_BATCH):
+                    quantise_en2(q)
+                    second_products(q, "bank")
+                    if q > 0:
+                        statistics(q - 1)
+                statistics(FIRST_BATCH - 1)
+            exponentials(g)
+            if g == FIRST_BATCH - 1:
+                for q in range(FIRST_BATCH):
+                    logarithm(q)
+
+        for q in range(FIRST_BATCH, CHUNKS):
+            logarithm(q)
+            quantise_en2(q)
+            second_products(q, "bank")
+            if q > FIRST_BATCH:
+                statistics(q - 1)
+        statistics(CHUNKS - 1)
+        nc.scalar.activation(out=warm[:], in_=one[:], func=ACT.Exp)
+
+        second_products(0, "acc")
+        second_products(1, "acc")
+        moments = keep.tile([P, 2, 2], F32)
+        for branch in range(2):
+            nc.vector.bn_aggr(out=moments[:, branch, :], in_=stats[:, branch, :, :].rearrange("p g s -> p (g s)"))
+        spread = keep.tile([P, 2], F32)
+        nc.gpsimd.tensor_scalar(
+            out=spread[:], in0=moments[:, :, 1], scalar1=1.0, scalar2=BN_EPS, op0=ALU.mult, op1=ALU.add
+        )
+        rstd = keep.tile([P, 2], F32)
+        nc.gpsimd.tensor_tensor(out=rstd[:], in0=spread[:], in1=neg_half[:], op=ALU.pow)
+        scale = keep.tile([P, 2], F32)
+        nc.gpsimd.tensor_tensor(out=scale[:], in0=rstd[:], in1=gain[:], op=ALU.mult)
+        centre = keep.tile([P, 2], F32)
+        nc.gpsimd.tensor_tensor(out=centre[:], in0=moments[:, :, 0], in1=scale[:], op=ALU.mult)
+        offset = keep.tile([P, 2], F32)
+        nc.gpsimd.tensor_tensor(out=offset[:], in0=shift[:], in1=centre[:], op=ALU.subtract)
+
+        for g in range(CHUNKS):
+            mean_t = tail_pool.tile([P, CHUNK], F32)
+            nc.scalar.activation(
+                out=mean_t[:], in_=heads[g][0][:], func=ACT.Identity, scale=scale[:, 0:1], bias=offset[:, 0:1]
+            )
+            dev_t = tail_pool.tile([P, CHUNK], F32)
+            nc.scalar.activation(
+                out=dev_t[:], in_=heads[g][1][:], func=ACT.Exp, scale=scale[:, 1:2], bias=offset[:, 1:2]
+            )
+            if g + 2 < CHUNKS:
+                second_products(g + 2, "acc")
+            mean_bank = psum.tile([P, CHUNK], F32, tag="bank")
+            dev_bank = psum.tile([P, CHUNK], F32, tag="bank")
+            for j in range(SUB):
+                nc.tensor.transpose(mean_bank[:, P * j : P * (j + 1)], mean_t[:, P * j : P * (j + 1)], ident[:])
+            for j in range(SUB):
+                nc.tensor.transpose(dev_bank[:, P * j : P * (j + 1)], dev_t[:, P * j : P * (j + 1)], ident[:])
+            noise = tail_pool.tile([P, CHUNK], F32)
+            nc.vector.tensor_tensor(out=noise[:], in0=dev_bank[:], in1=eps_rows[:, g, :], op=ALU.mult)
+            z = tail_pool.tile([P, CHUNK], F32)
+            nc.vector.tensor_tensor(out=z[:], in0=mean_bank[:], in1=noise[:], op=ALU.add)
+            nc.sync.dma_start(out=out_chunks[g], in_=z[:])

@@ -19,30 +19,31 @@ CHUNKS = ROWS // CHUNK
 SUB = CHUNK // P
 PASSES = K1 // (P * PACK)
 HALF = CHUNK // 2
+ROW_WORDS = K1 // 2
 BN_EPS = 1e-5
 
-FIRST_BATCH = 2
 LEAD = 2
-RAW_BUFS = 4
+RAW_BUFS = 3
+AHEAD = 2
 
 FLOPS = 2 * ROWS * K1 * HIDDEN + 2 * 2 * ROWS * HIDDEN * OUTS
 
 
 def tile_model_pa_t_kernel(tc, en1, eps, W2, b2, Wm, Wv, gm, betam, gv, betav, out):
     nc = tc.nc
-    en1_chunks = en1.rearrange("(g p j) k -> g p (j k)", p=P, j=SUB)
-    w2_rows = W2.rearrange("(p j) k -> p (j k)", j=SUB)
+    en1_halves = en1.rearrange("(g p h j) k -> g h p (j k)", p=P, h=2, j=2)
+    w2_halves = W2.rearrange("(p h j) k -> h p (j k)", h=2, j=2)
     eps_chunks = eps.rearrange("(g p j) c -> p g (j c)", p=P, j=SUB)
     out_chunks = out.rearrange("(g p j) c -> g p (j c)", p=P, j=SUB)
 
     with ExitStack() as ctx:
         ctx.enter_context(tc.manual_schedule())
         keep = ctx.enter_context(tc.tile_pool(name="keep", bufs=1))
-        raw_pool = ctx.enter_context(tc.tile_pool(name="raw", bufs=RAW_BUFS))
-        grouped_pool = ctx.enter_context(tc.tile_pool(name="grouped", bufs=4))
-        codes_pool = ctx.enter_context(tc.tile_pool(name="codes", bufs=LEAD + 3))
-        exp_pool = ctx.enter_context(tc.tile_pool(name="exp", bufs=max(FIRST_BATCH, CHUNKS - FIRST_BATCH)))
-        en2_pool = ctx.enter_context(tc.tile_pool(name="en2", bufs=4))
+        raw_pool = ctx.enter_context(tc.tile_pool(name="raw", bufs=2 * RAW_BUFS))
+        grouped_pool = ctx.enter_context(tc.tile_pool(name="grouped", bufs=8))
+        codes_pool = ctx.enter_context(tc.tile_pool(name="codes", bufs=LEAD + 2))
+        exp_pool = ctx.enter_context(tc.tile_pool(name="exp", bufs=CHUNKS))
+        en2_pool = ctx.enter_context(tc.tile_pool(name="en2", bufs=3))
         en2_codes_pool = ctx.enter_context(tc.tile_pool(name="en2codes", bufs=CHUNKS))
         tail_pool = ctx.enter_context(tc.tile_pool(name="tail", bufs=3))
         psum = ctx.enter_context(tc.psum_pool(name="psum", bufs=4))
@@ -59,22 +60,6 @@ def tile_model_pa_t_kernel(tc, en1, eps, W2, b2, Wm, Wv, gm, betam, gv, betav, o
         en2_scales = {}
         heads = {}
 
-        def load_chunk(g):
-            x_raw = raw_pool.tile([P, SUB * K1], BF16)
-            nc.sync.dma_start(out=x_raw[:], in_=en1_chunks[g])
-            raw[g] = x_raw
-
-        load_chunk(0)
-        w2_raw = keep.tile([P, SUB * K1], BF16)
-        nc.sync.dma_start(out=w2_raw[:], in_=w2_rows)
-        raw["w2"] = w2_raw
-        wm_raw = keep.tile([P, HIDDEN], BF16)
-        nc.sync.dma_start(out=wm_raw[:], in_=Wm)
-        wv_raw = keep.tile([P, HIDDEN], BF16)
-        nc.sync.dma_start(out=wv_raw[:], in_=Wv)
-        for g in range(1, RAW_BUFS):
-            load_chunk(g)
-
         b2_raw = keep.tile([P, PACK], BF16)
         gm_raw = keep.tile([P, 1], BF16)
         gv_raw = keep.tile([P, 1], BF16)
@@ -86,6 +71,19 @@ def tile_model_pa_t_kernel(tc, en1, eps, W2, b2, Wm, Wv, gm, betam, gv, betav, o
             nc.scalar.dma_start(out=gv_raw[:], in_=gv.rearrange("(p o) -> p o", o=1))
             nc.scalar.dma_start(out=betam_raw[:], in_=betam.rearrange("(p o) -> p o", o=1))
             nc.scalar.dma_start(out=betav_raw[:], in_=betav.rearrange("(p o) -> p o", o=1))
+
+        def load_chunk(g):
+            for h in range(2):
+                x_raw = raw_pool.tile([P, 2 * K1], BF16)
+                nc.sync.dma_start(out=x_raw[:], in_=en1_halves[g, h])
+                raw[(g, h)] = x_raw
+
+        for h in range(2):
+            w2_raw = keep.tile([P, 2 * K1], BF16, tag="w2_raw%d" % h)
+            nc.sync.dma_start(out=w2_raw[:], in_=w2_halves[h])
+            raw[("w2", h)] = w2_raw
+        for g in range(RAW_BUFS):
+            load_chunk(g)
 
         one = keep.tile([P, 1], F32)
         nc.vector.memset(one[:], 1.0)
@@ -106,13 +104,13 @@ def tile_model_pa_t_kernel(tc, en1, eps, W2, b2, Wm, Wv, gm, betam, gv, betav, o
         nc.gpsimd.tensor_scalar(out=shift[:, 1:2], in0=betav_raw[:], scalar1=0.5, scalar2=0.0, op0=ALU.mult, op1=ALU.add)
 
         def transpose_block(block):
-            words = raw[block][:].bitcast(F32)
-            for c in range(PASSES):
-                for h in range(2):
+            for h in range(2):
+                words = raw[(block, h)][:].bitcast(F32)
+                for c in range(PASSES):
                     bank = psum.tile([P, CHUNK], F32, tag="bank")
                     for jj in range(2):
                         for u in range(2):
-                            first = (2 * h + jj) * (K1 // 2) + 256 * c + P * u
+                            first = ROW_WORDS * jj + 2 * P * c + P * u
                             nc.tensor.transpose(
                                 bank[:, HALF * u + P * jj : HALF * u + P * (jj + 1)],
                                 words[:, first : first + P],
@@ -120,69 +118,41 @@ def tile_model_pa_t_kernel(tc, en1, eps, W2, b2, Wm, Wv, gm, betam, gv, betav, o
                             )
                     banks[(block, c, h)] = bank
 
-        def open_block(block, pool):
-            for c in range(PASSES):
-                pass_in = grouped_pool.tile([P, CHUNK * PACK], BF16, align_bytes=64, tag="grouped")
-                grouped[(block, c)] = pass_in
+        def copy_out(copy, block):
+            for h in range(2):
+                for c in range(PASSES):
+                    bank_in = grouped_pool.tile([P, HALF * PACK], BF16, align_bytes=64, tag="grouped")
+                    copy(
+                        out=bank_in[:].bitcast(F32).rearrange("p (r u) -> p r u", u=2),
+                        in_=banks[(block, c, h)][:].rearrange("p (u r) -> p r u", u=2),
+                    )
+                    grouped[(block, c, h)] = bank_in
+
+        def quantise_block(block, pool):
             block_codes = pool.tile([P, PASSES, CHUNK], U32, align_bytes=64, tag="codes")
             block_scales = pool.tile([P, PASSES, CHUNK], U8, align_bytes=64, tag="scales")
+            for h in range(2):
+                for c in range(PASSES):
+                    nc.vector.quantize_mx(
+                        out=block_codes[:, c, HALF * h : HALF * (h + 1)].bitcast(FP8X4),
+                        scales=block_scales[:, c, HALF * h : HALF * (h + 1)],
+                        in_=grouped[(block, c, h)][:],
+                    )
             codes[block] = block_codes
             scales[block] = block_scales
 
-        def copy_out(copy, block, c, h):
-            words = grouped[(block, c)][:].bitcast(F32)
-            copy(
-                out=words[:, CHUNK * h : CHUNK * (h + 1)].rearrange("p (r u) -> p r u", u=2),
-                in_=banks[(block, c, h)][:].rearrange("p (u r) -> p r u", u=2),
-            )
-
-        def quantise(block, c):
-            nc.vector.quantize_mx(
-                out=codes[block][:, c, :].bitcast(FP8X4),
-                scales=scales[block][:, c, :],
-                in_=grouped[(block, c)][:],
-            )
-
-        def front(g, late):
+        def front(g):
             transpose_block(g)
             if g + RAW_BUFS < CHUNKS:
                 load_chunk(g + RAW_BUFS)
-            open_block(g, codes_pool)
-            copy_out(nc.vector.tensor_copy, g, 0, 0)
-            if late is not None:
-                quantise(late, 1)
-            copy_out(nc.vector.tensor_copy, g, 0, 1)
-            copy_out(nc.vector.tensor_copy, g, 1, 0)
-            quantise(g, 0)
-            copy_out(nc.vector.tensor_copy, g, 1, 1)
-
-        front(0, None)
+            copy_out(nc.vector.tensor_copy, g)
+            quantise_block(g, codes_pool)
 
         transpose_block("w2")
-        open_block("w2", keep)
-        for c in range(PASSES):
-            for h in range(2):
-                copy_out(nc.scalar.copy, "w2", c, h)
-        head_bank = psum.tile([P, CHUNK], F32, tag="bank")
-        for branch, head_raw in enumerate((wm_raw, wv_raw)):
-            planes = head_raw[:].bitcast(F32).rearrange("p (q u) -> p u q", u=2)
-            for u in range(2):
-                nc.tensor.transpose(
-                    head_bank[:, HALF * u + P * branch : HALF * u + P * (branch + 1)], planes[:, u, :], ident[:]
-                )
-        head_grouped = keep.tile([P, 2 * OUTS * PACK], BF16, align_bytes=64)
-        nc.scalar.copy(
-            out=head_grouped[:].bitcast(F32).rearrange("p (r u) -> p r u", u=2),
-            in_=head_bank[:].rearrange("p (u r) -> p r u", u=2),
-        )
-        head_codes = keep.tile([P, 2 * OUTS], U32, align_bytes=64)
-        head_scales = keep.tile([P, 2 * OUTS], U8, align_bytes=64)
-        quantise("w2", 0)
-        quantise(0, 1)
-        quantise("w2", 1)
-        nc.vector.quantize_mx(out=head_codes[:].bitcast(FP8X4), scales=head_scales[:], in_=head_grouped[:])
-
-        front(1, None)
+        copy_out(nc.scalar.copy, "w2")
+        quantise_block("w2", keep)
+        for g in range(LEAD):
+            front(g)
 
         def first_product(g):
             for m in range(PACK):
@@ -204,6 +174,35 @@ def tile_model_pa_t_kernel(tc, en1, eps, W2, b2, Wm, Wv, gm, betam, gv, betav, o
             for m in range(PACK):
                 nc.scalar.activation(out=e[:, m, :], in_=sums[(g, m)][:], func=ACT.Exp, bias=b2_f32[:, m : m + 1])
             expo[g] = e
+
+        for g in range(CHUNKS):
+            first_product(g)
+            if g + LEAD < CHUNKS:
+                front(g + LEAD)
+            exponentials(g)
+
+        wm_raw = keep.tile([P, HIDDEN], BF16)
+        nc.sync.dma_start(out=wm_raw[:], in_=Wm)
+        wv_raw = keep.tile([P, HIDDEN], BF16)
+        nc.sync.dma_start(out=wv_raw[:], in_=Wv)
+        eps_rows = keep.tile([P, CHUNKS, CHUNK], BF16)
+        nc.sync.dma_start(out=eps_rows[:], in_=eps_chunks)
+
+        head_bank = psum.tile([P, CHUNK], F32, tag="bank")
+        for branch, head_raw in enumerate((wm_raw, wv_raw)):
+            planes = head_raw[:].bitcast(F32).rearrange("p (q u) -> p u q", u=2)
+            for u in range(2):
+                nc.tensor.transpose(
+                    head_bank[:, HALF * u + P * branch : HALF * u + P * (branch + 1)], planes[:, u, :], ident[:]
+                )
+        head_grouped = keep.tile([P, 2 * OUTS * PACK], BF16, align_bytes=64)
+        nc.vector.tensor_copy(
+            out=head_grouped[:].bitcast(F32).rearrange("p (r u) -> p r u", u=2),
+            in_=head_bank[:].rearrange("p (u r) -> p r u", u=2),
+        )
+        head_codes = keep.tile([P, 2 * OUTS], U32, align_bytes=64)
+        head_scales = keep.tile([P, 2 * OUTS], U8, align_bytes=64)
+        nc.vector.quantize_mx(out=head_codes[:].bitcast(FP8X4), scales=head_scales[:], in_=head_grouped[:])
 
         def logarithm(g):
             soft = en2_pool.tile([P, CHUNK * PACK], BF16, align_bytes=64)
@@ -244,37 +243,17 @@ def tile_model_pa_t_kernel(tc, en1, eps, W2, b2, Wm, Wv, gm, betam, gv, betav, o
             for branch in range(2):
                 nc.vector.bn_stats(out=stats[:, branch, g, :], in_=heads[g][branch][:])
 
-        eps_rows = keep.tile([P, CHUNKS, CHUNK], BF16)
         for g in range(CHUNKS):
-            if g + LEAD < CHUNKS:
-                front(g + LEAD, g + LEAD - 1)
-            elif g + LEAD == CHUNKS:
-                quantise(CHUNKS - 1, 1)
-                nc.sync.dma_start(out=eps_rows[:], in_=eps_chunks)
-            first_product(g)
-            if g == FIRST_BATCH:
-                for q in range(FIRST_BATCH):
-                    quantise_en2(q)
-                    second_products(q, "bank")
-                    if q > 0:
-                        statistics(q - 1)
-                statistics(FIRST_BATCH - 1)
-            exponentials(g)
-            if g == FIRST_BATCH - 1:
-                for q in range(FIRST_BATCH):
-                    logarithm(q)
-
-        for q in range(FIRST_BATCH, CHUNKS):
-            logarithm(q)
-            quantise_en2(q)
-            second_products(q, "bank")
-            if q > FIRST_BATCH:
-                statistics(q - 1)
+            logarithm(g)
+            quantise_en2(g)
+            second_products(g, "bank")
+            if g > 0:
+                statistics(g - 1)
         statistics(CHUNKS - 1)
         nc.scalar.activation(out=warm[:], in_=one[:], func=ACT.Exp)
 
-        second_products(0, "acc")
-        second_products(1, "acc")
+        for g in range(AHEAD):
+            second_products(g, "acc")
         moments = keep.tile([P, 2, 2], F32)
         for branch in range(2):
             nc.vector.bn_aggr(out=moments[:, branch, :], in_=stats[:, branch, :, :].rearrange("p g s -> p (g s)"))
@@ -300,8 +279,8 @@ def tile_model_pa_t_kernel(tc, en1, eps, W2, b2, Wm, Wv, gm, betam, gv, betav, o
             nc.scalar.activation(
                 out=dev_t[:], in_=heads[g][1][:], func=ACT.Exp, scale=scale[:, 1:2], bias=offset[:, 1:2]
             )
-            if g + 2 < CHUNKS:
-                second_products(g + 2, "acc")
+            if g + AHEAD < CHUNKS:
+                second_products(g + AHEAD, "acc")
             mean_bank = psum.tile([P, CHUNK], F32, tag="bank")
             dev_bank = psum.tile([P, CHUNK], F32, tag="bank")
             for j in range(SUB):

@@ -22,7 +22,10 @@ HALF = CHUNK // 2
 ROW_WORDS = K1 // 2
 BN_EPS = 1e-5
 
+FIRST_BATCH = 3
 LEAD = 2
+LEAD_LATE = 4
+SPINS_AT_START = 6
 RAW_BUFS = 3
 AHEAD = 2
 
@@ -41,9 +44,9 @@ def tile_model_pa_t_kernel(tc, en1, eps, W2, b2, Wm, Wv, gm, betam, gv, betav, o
         keep = ctx.enter_context(tc.tile_pool(name="keep", bufs=1))
         raw_pool = ctx.enter_context(tc.tile_pool(name="raw", bufs=2 * RAW_BUFS))
         grouped_pool = ctx.enter_context(tc.tile_pool(name="grouped", bufs=8))
-        codes_pool = ctx.enter_context(tc.tile_pool(name="codes", bufs=LEAD + 2))
-        exp_pool = ctx.enter_context(tc.tile_pool(name="exp", bufs=CHUNKS))
-        en2_pool = ctx.enter_context(tc.tile_pool(name="en2", bufs=3))
+        codes_pool = ctx.enter_context(tc.tile_pool(name="codes", bufs=LEAD_LATE + 2))
+        exp_pool = ctx.enter_context(tc.tile_pool(name="exp", bufs=max(FIRST_BATCH, CHUNKS - FIRST_BATCH)))
+        en2_pool = ctx.enter_context(tc.tile_pool(name="en2", bufs=FIRST_BATCH + 3))
         en2_codes_pool = ctx.enter_context(tc.tile_pool(name="en2codes", bufs=CHUNKS))
         tail_pool = ctx.enter_context(tc.tile_pool(name="tail", bufs=3))
         psum = ctx.enter_context(tc.psum_pool(name="psum", bufs=4))
@@ -78,12 +81,23 @@ def tile_model_pa_t_kernel(tc, en1, eps, W2, b2, Wm, Wv, gm, betam, gv, betav, o
                 nc.sync.dma_start(out=x_raw[:], in_=en1_halves[g, h])
                 raw[(g, h)] = x_raw
 
+        load_chunk(0)
         for h in range(2):
             w2_raw = keep.tile([P, 2 * K1], BF16, tag="w2_raw%d" % h)
             nc.sync.dma_start(out=w2_raw[:], in_=w2_halves[h])
             raw[("w2", h)] = w2_raw
-        for g in range(RAW_BUFS):
+        for g in range(1, RAW_BUFS):
             load_chunk(g)
+
+        zeros = keep.tile([P, CHUNK], BF16)
+        nc.vector.memset(zeros[:], 0.0)
+        unread = psum.tile([P, CHUNK], F32, tag="acc")
+
+        def spin(count):
+            for i in range(count):
+                nc.tensor.matmul(out=unread[:], lhsT=zeros[:, 0:P], rhs=zeros[:], start=True, stop=True)
+
+        spin(SPINS_AT_START)
 
         one = keep.tile([P, 1], F32)
         nc.vector.memset(one[:], 1.0)
@@ -103,7 +117,7 @@ def tile_model_pa_t_kernel(tc, en1, eps, W2, b2, Wm, Wv, gm, betam, gv, betav, o
         nc.gpsimd.tensor_copy(out=shift[:, 0:1], in_=betam_raw[:])
         nc.gpsimd.tensor_scalar(out=shift[:, 1:2], in0=betav_raw[:], scalar1=0.5, scalar2=0.0, op0=ALU.mult, op1=ALU.add)
 
-        def transpose_block(block):
+        def transpose_block(block, spins=0):
             for h in range(2):
                 words = raw[(block, h)][:].bitcast(F32)
                 for c in range(PASSES):
@@ -117,6 +131,7 @@ def tile_model_pa_t_kernel(tc, en1, eps, W2, b2, Wm, Wv, gm, betam, gv, betav, o
                                 ident[:],
                             )
                     banks[(block, c, h)] = bank
+                spin(spins)
 
         def copy_out(copy, block):
             for h in range(2):
@@ -141,18 +156,19 @@ def tile_model_pa_t_kernel(tc, en1, eps, W2, b2, Wm, Wv, gm, betam, gv, betav, o
             codes[block] = block_codes
             scales[block] = block_scales
 
-        def front(g):
-            transpose_block(g)
+        def front(g, spins=0):
+            transpose_block(g, spins)
             if g + RAW_BUFS < CHUNKS:
                 load_chunk(g + RAW_BUFS)
             copy_out(nc.vector.tensor_copy, g)
             quantise_block(g, codes_pool)
 
-        transpose_block("w2")
+        front(0, spins=1)
+        transpose_block("w2", spins=1)
         copy_out(nc.scalar.copy, "w2")
         quantise_block("w2", keep)
-        for g in range(LEAD):
-            front(g)
+        for g in range(1, LEAD):
+            front(g, spins=1)
 
         def first_product(g):
             for m in range(PACK):
@@ -175,11 +191,27 @@ def tile_model_pa_t_kernel(tc, en1, eps, W2, b2, Wm, Wv, gm, betam, gv, betav, o
                 nc.scalar.activation(out=e[:, m, :], in_=sums[(g, m)][:], func=ACT.Exp, bias=b2_f32[:, m : m + 1])
             expo[g] = e
 
+        def logarithm(g):
+            soft = en2_pool.tile([P, CHUNK * PACK], BF16, align_bytes=64)
+            nc.scalar.activation(
+                out=soft[:].rearrange("p (q i t) -> p q t i", i=4, t=PACK),
+                in_=expo[g][:].rearrange("p t (q i) -> p q t i", i=4),
+                func=ACT.Ln,
+                bias=one[:],
+            )
+            en2[g] = soft
+
+        fronts = LEAD
         for g in range(CHUNKS):
             first_product(g)
-            if g + LEAD < CHUNKS:
-                front(g + LEAD)
+            wanted = min(CHUNKS, g + 1 + (LEAD if g < FIRST_BATCH - 1 else LEAD_LATE))
+            for ahead in range(fronts, wanted):
+                front(ahead)
+            fronts = max(fronts, wanted)
             exponentials(g)
+            if g == FIRST_BATCH - 1:
+                for q in range(FIRST_BATCH):
+                    logarithm(q)
 
         wm_raw = keep.tile([P, HIDDEN], BF16)
         nc.sync.dma_start(out=wm_raw[:], in_=Wm)
@@ -203,16 +235,6 @@ def tile_model_pa_t_kernel(tc, en1, eps, W2, b2, Wm, Wv, gm, betam, gv, betav, o
         head_codes = keep.tile([P, 2 * OUTS], U32, align_bytes=64)
         head_scales = keep.tile([P, 2 * OUTS], U8, align_bytes=64)
         nc.vector.quantize_mx(out=head_codes[:].bitcast(FP8X4), scales=head_scales[:], in_=head_grouped[:])
-
-        def logarithm(g):
-            soft = en2_pool.tile([P, CHUNK * PACK], BF16, align_bytes=64)
-            nc.scalar.activation(
-                out=soft[:].rearrange("p (q i t) -> p q t i", i=4, t=PACK),
-                in_=expo[g][:].rearrange("p t (q i) -> p q t i", i=4),
-                func=ACT.Ln,
-                bias=one[:],
-            )
-            en2[g] = soft
 
         def quantise_en2(g):
             soft_codes = en2_codes_pool.tile([P, CHUNK], U32, align_bytes=64)
@@ -244,7 +266,8 @@ def tile_model_pa_t_kernel(tc, en1, eps, W2, b2, Wm, Wv, gm, betam, gv, betav, o
                 nc.vector.bn_stats(out=stats[:, branch, g, :], in_=heads[g][branch][:])
 
         for g in range(CHUNKS):
-            logarithm(g)
+            if g >= FIRST_BATCH:
+                logarithm(g)
             quantise_en2(g)
             second_products(g, "bank")
             if g > 0:

@@ -23,11 +23,11 @@ ROW_WORDS = K1 // 2
 BN_EPS = 1e-5
 
 FIRST_BATCH = 3
-LEAD = 2
-LEAD_LATE = 4
 SPINS_AT_START = 6
 RAW_BUFS = 3
-AHEAD = 2
+LAST = CHUNKS - 1
+KEPT = 2
+MEAN, VAR = 0, 1
 
 FLOPS = 2 * ROWS * K1 * HIDDEN + 2 * 2 * ROWS * HIDDEN * OUTS
 
@@ -35,7 +35,7 @@ FLOPS = 2 * ROWS * K1 * HIDDEN + 2 * 2 * ROWS * HIDDEN * OUTS
 def tile_model_pa_t_kernel(tc, en1, eps, W2, b2, Wm, Wv, gm, betam, gv, betav, out):
     nc = tc.nc
     en1_halves = en1.rearrange("(g p h j) k -> g h p (j k)", p=P, h=2, j=2)
-    w2_halves = W2.rearrange("(p h j) k -> h p (j k)", h=2, j=2)
+    w2_slabs = W2.rearrange("(p m) k -> m p k", m=PACK)
     eps_chunks = eps.rearrange("(g p j) c -> p g (j c)", p=P, j=SUB)
     out_chunks = out.rearrange("(g p j) c -> g p (j c)", p=P, j=SUB)
 
@@ -44,7 +44,7 @@ def tile_model_pa_t_kernel(tc, en1, eps, W2, b2, Wm, Wv, gm, betam, gv, betav, o
         keep = ctx.enter_context(tc.tile_pool(name="keep", bufs=1))
         raw_pool = ctx.enter_context(tc.tile_pool(name="raw", bufs=2 * RAW_BUFS))
         grouped_pool = ctx.enter_context(tc.tile_pool(name="grouped", bufs=8))
-        codes_pool = ctx.enter_context(tc.tile_pool(name="codes", bufs=LEAD_LATE + 2))
+        codes_pool = ctx.enter_context(tc.tile_pool(name="codes", bufs=6))
         exp_pool = ctx.enter_context(tc.tile_pool(name="exp", bufs=max(FIRST_BATCH, CHUNKS - FIRST_BATCH)))
         en2_pool = ctx.enter_context(tc.tile_pool(name="en2", bufs=FIRST_BATCH + 3))
         en2_codes_pool = ctx.enter_context(tc.tile_pool(name="en2codes", bufs=CHUNKS))
@@ -56,11 +56,13 @@ def tile_model_pa_t_kernel(tc, en1, eps, W2, b2, Wm, Wv, gm, betam, gv, betav, o
         grouped = {}
         codes = {}
         scales = {}
+        w2_banks = {}
+        w2_grouped = {}
+        w2_codes = {}
+        w2_scales = {}
         sums = {}
         expo = {}
         en2 = {}
-        en2_codes = {}
-        en2_scales = {}
         heads = {}
 
         b2_raw = keep.tile([P, PACK], BF16)
@@ -81,11 +83,11 @@ def tile_model_pa_t_kernel(tc, en1, eps, W2, b2, Wm, Wv, gm, betam, gv, betav, o
                 nc.sync.dma_start(out=x_raw[:], in_=en1_halves[g, h])
                 raw[(g, h)] = x_raw
 
+        w2_raw = [keep.tile([P, K1], BF16, tag="w2_raw%d" % m, name="w2_raw%d" % m) for m in range(PACK)]
+        nc.sync.dma_start(out=w2_raw[0][:], in_=w2_slabs[0])
         load_chunk(0)
-        for h in range(2):
-            w2_raw = keep.tile([P, 2 * K1], BF16, tag="w2_raw%d" % h)
-            nc.sync.dma_start(out=w2_raw[:], in_=w2_halves[h])
-            raw[("w2", h)] = w2_raw
+        for m in range(1, PACK):
+            nc.sync.dma_start(out=w2_raw[m][:], in_=w2_slabs[m])
         for g in range(1, RAW_BUFS):
             load_chunk(g)
 
@@ -111,64 +113,99 @@ def tile_model_pa_t_kernel(tc, en1, eps, W2, b2, Wm, Wv, gm, betam, gv, betav, o
         b2_f32 = keep.tile([P, PACK], F32)
         nc.gpsimd.tensor_copy(out=b2_f32[:], in_=b2_raw[:])
         gain = keep.tile([P, 2], F32)
+        neg_gain = keep.tile([P, 2], F32)
         shift = keep.tile([P, 2], F32)
         nc.gpsimd.tensor_copy(out=gain[:, 0:1], in_=gm_raw[:])
         nc.gpsimd.tensor_scalar(out=gain[:, 1:2], in0=gv_raw[:], scalar1=0.5, scalar2=0.0, op0=ALU.mult, op1=ALU.add)
+        nc.gpsimd.tensor_scalar(out=neg_gain[:], in0=gain[:], scalar1=-1.0, scalar2=0.0, op0=ALU.mult, op1=ALU.add)
         nc.gpsimd.tensor_copy(out=shift[:, 0:1], in_=betam_raw[:])
         nc.gpsimd.tensor_scalar(out=shift[:, 1:2], in0=betav_raw[:], scalar1=0.5, scalar2=0.0, op0=ALU.mult, op1=ALU.add)
 
-        def transpose_block(block, spins=0):
-            for h in range(2):
-                words = raw[(block, h)][:].bitcast(F32)
-                for c in range(PASSES):
-                    bank = psum.tile([P, CHUNK], F32, tag="bank")
-                    for jj in range(2):
-                        for u in range(2):
-                            first = ROW_WORDS * jj + 2 * P * c + P * u
-                            nc.tensor.transpose(
-                                bank[:, HALF * u + P * jj : HALF * u + P * (jj + 1)],
-                                words[:, first : first + P],
-                                ident[:],
-                            )
-                    banks[(block, c, h)] = bank
-                spin(spins)
+        def transpose_slab(m):
+            words = w2_raw[m][:].bitcast(F32)
+            bank = psum.tile([P, CHUNK], F32, tag="bank")
+            for plane in range(2 * PASSES):
+                nc.tensor.transpose(
+                    bank[:, P * plane : P * (plane + 1)], words[:, P * plane : P * (plane + 1)], ident[:]
+                )
+            w2_banks[m] = bank
 
-        def copy_out(copy, block):
-            for h in range(2):
-                for c in range(PASSES):
-                    bank_in = grouped_pool.tile([P, HALF * PACK], BF16, align_bytes=64, tag="grouped")
-                    copy(
-                        out=bank_in[:].bitcast(F32).rearrange("p (r u) -> p r u", u=2),
-                        in_=banks[(block, c, h)][:].rearrange("p (u r) -> p r u", u=2),
-                    )
-                    grouped[(block, c, h)] = bank_in
+        def copy_slab(m):
+            slab_in = grouped_pool.tile([P, HALF * PACK], BF16, align_bytes=64, tag="grouped")
+            nc.scalar.copy(
+                out=slab_in[:].bitcast(F32).rearrange("p (c r u) -> p c r u", c=PASSES, u=2),
+                in_=w2_banks[m][:].rearrange("p (c u r) -> p c r u", c=PASSES, u=2),
+            )
+            w2_grouped[m] = slab_in
 
-        def quantise_block(block, pool):
-            block_codes = pool.tile([P, PASSES, CHUNK], U32, align_bytes=64, tag="codes")
-            block_scales = pool.tile([P, PASSES, CHUNK], U8, align_bytes=64, tag="scales")
-            for h in range(2):
-                for c in range(PASSES):
-                    nc.vector.quantize_mx(
-                        out=block_codes[:, c, HALF * h : HALF * (h + 1)].bitcast(FP8X4),
-                        scales=block_scales[:, c, HALF * h : HALF * (h + 1)],
-                        in_=grouped[(block, c, h)][:],
-                    )
-            codes[block] = block_codes
-            scales[block] = block_scales
+        def quantise_slab(m):
+            slab_codes = keep.tile([P, PASSES, P], U32, align_bytes=64, tag="w2_codes%d" % m)
+            slab_scales = keep.tile([P, PASSES, P], U8, align_bytes=64, tag="w2_scales%d" % m)
+            nc.vector.quantize_mx(
+                out=slab_codes[:].rearrange("p c r -> p (c r)").bitcast(FP8X4),
+                scales=slab_scales[:].rearrange("p c r -> p (c r)"),
+                in_=w2_grouped[m][:],
+            )
+            w2_codes[m] = slab_codes
+            w2_scales[m] = slab_scales
 
-        def front(g, spins=0):
-            transpose_block(g, spins)
+        def transpose_half(g, h):
+            words = raw[(g, h)][:].bitcast(F32)
+            for c in range(PASSES):
+                bank = psum.tile([P, CHUNK], F32, tag="bank")
+                for jj in range(2):
+                    for u in range(2):
+                        first = ROW_WORDS * jj + 2 * P * c + P * u
+                        nc.tensor.transpose(
+                            bank[:, HALF * u + P * jj : HALF * u + P * (jj + 1)],
+                            words[:, first : first + P],
+                            ident[:],
+                        )
+                banks[(g, c, h)] = bank
+
+        def copy_bank(copy, g, c, h):
+            bank_in = grouped_pool.tile([P, HALF * PACK], BF16, align_bytes=64, tag="grouped")
+            copy(
+                out=bank_in[:].bitcast(F32).rearrange("p (r u) -> p r u", u=2),
+                in_=banks[(g, c, h)][:].rearrange("p (u r) -> p r u", u=2),
+            )
+            grouped[(g, c, h)] = bank_in
+
+        def open_codes(g):
+            chunk_codes = codes_pool.tile([P, PASSES, CHUNK], U32, align_bytes=64)
+            chunk_scales = codes_pool.tile([P, PASSES, CHUNK], U8, align_bytes=64)
+            codes[g] = chunk_codes
+            scales[g] = chunk_scales
+
+        def quantise_bank(g, c, h):
+            nc.vector.quantize_mx(
+                out=codes[g][:, c, HALF * h : HALF * (h + 1)].bitcast(FP8X4),
+                scales=scales[g][:, c, HALF * h : HALF * (h + 1)],
+                in_=grouped[(g, c, h)][:],
+            )
+
+        def front(g):
+            for h in range(2):
+                transpose_half(g, h)
             if g + RAW_BUFS < CHUNKS:
                 load_chunk(g + RAW_BUFS)
-            copy_out(nc.vector.tensor_copy, g)
-            quantise_block(g, codes_pool)
+            for h in range(2):
+                for c in range(PASSES):
+                    copy_bank(nc.scalar.copy if c == 1 and g < FIRST_BATCH else nc.vector.tensor_copy, g, c, h)
+            open_codes(g)
+            for h in range(2):
+                for c in range(PASSES):
+                    quantise_bank(g, c, h)
 
-        front(0, spins=1)
-        transpose_block("w2", spins=1)
-        copy_out(nc.scalar.copy, "w2")
-        quantise_block("w2", keep)
-        for g in range(1, LEAD):
-            front(g, spins=1)
+        transpose_slab(0)
+        copy_slab(0)
+        quantise_slab(0)
+        front(0)
+        for m in range(1, PACK):
+            transpose_slab(m)
+            copy_slab(m)
+        for m in range(1, PACK):
+            quantise_slab(m)
 
         def first_product(g):
             for m in range(PACK):
@@ -176,8 +213,8 @@ def tile_model_pa_t_kernel(tc, en1, eps, W2, b2, Wm, Wv, gm, betam, gv, betav, o
                 for c in range(PASSES):
                     nc.tensor.matmul_mx(
                         out=acc[:],
-                        lhsT=codes["w2"][:, c, P * m : P * (m + 1)].bitcast(FP8X4),
-                        lhsT_scale=scales["w2"][:, c, P * m : P * (m + 1)],
+                        lhsT=w2_codes[m][:, c, :].bitcast(FP8X4),
+                        lhsT_scale=w2_scales[m][:, c, :],
                         rhs=codes[g][:, c, :].bitcast(FP8X4),
                         rhs_scale=scales[g][:, c, :],
                         start=(c == 0),
@@ -191,24 +228,24 @@ def tile_model_pa_t_kernel(tc, en1, eps, W2, b2, Wm, Wv, gm, betam, gv, betav, o
                 nc.scalar.activation(out=e[:, m, :], in_=sums[(g, m)][:], func=ACT.Exp, bias=b2_f32[:, m : m + 1])
             expo[g] = e
 
-        def logarithm(g):
-            soft = en2_pool.tile([P, CHUNK * PACK], BF16, align_bytes=64)
+        def logarithm(g, half=None):
+            if half in (None, 0):
+                soft = en2_pool.tile([P, CHUNK * PACK], BF16, align_bytes=64)
+                en2[g] = soft
+            cols = slice(0, CHUNK) if half is None else slice(HALF * half, HALF * (half + 1))
             nc.scalar.activation(
-                out=soft[:].rearrange("p (q i t) -> p q t i", i=4, t=PACK),
-                in_=expo[g][:].rearrange("p t (q i) -> p q t i", i=4),
+                out=en2[g][:, PACK * cols.start : PACK * cols.stop].rearrange("p (q i t) -> p q t i", i=4, t=PACK),
+                in_=expo[g][:, :, cols].rearrange("p t (q i) -> p q t i", i=4),
                 func=ACT.Ln,
                 bias=one[:],
             )
-            en2[g] = soft
 
-        fronts = LEAD
+        fronts = {0: (1, 2), FIRST_BATCH - 1: (3, 4), FIRST_BATCH: (5, 6, 7)}
         for g in range(CHUNKS):
             first_product(g)
-            wanted = min(CHUNKS, g + 1 + (LEAD if g < FIRST_BATCH - 1 else LEAD_LATE))
-            for ahead in range(fronts, wanted):
-                front(ahead)
-            fronts = max(fronts, wanted)
             exponentials(g)
+            for ahead in fronts.get(g, ()):
+                front(ahead)
             if g == FIRST_BATCH - 1:
                 for q in range(FIRST_BATCH):
                     logarithm(q)
@@ -236,82 +273,169 @@ def tile_model_pa_t_kernel(tc, en1, eps, W2, b2, Wm, Wv, gm, betam, gv, betav, o
         head_scales = keep.tile([P, 2 * OUTS], U8, align_bytes=64)
         nc.vector.quantize_mx(out=head_codes[:].bitcast(FP8X4), scales=head_scales[:], in_=head_grouped[:])
 
-        def quantise_en2(g):
-            soft_codes = en2_codes_pool.tile([P, CHUNK], U32, align_bytes=64)
-            soft_scales = en2_codes_pool.tile([P, CHUNK], U8, align_bytes=64)
-            nc.vector.quantize_mx(out=soft_codes[:].bitcast(FP8X4), scales=soft_scales[:], in_=en2[g][:])
-            en2_codes[g] = soft_codes
-            en2_scales[g] = soft_scales
+        en2_codes = {}
+        en2_scales = {}
+
+        def quantise_en2(g, half=None):
+            if half in (None, 0):
+                soft_codes = en2_codes_pool.tile([P, CHUNK], U32, align_bytes=64)
+                soft_scales = en2_codes_pool.tile([P, CHUNK], U8, align_bytes=64)
+                en2_codes[g] = soft_codes
+                en2_scales[g] = soft_scales
+            cols = slice(0, CHUNK) if half is None else slice(HALF * half, HALF * (half + 1))
+            nc.vector.quantize_mx(
+                out=en2_codes[g][:, cols].bitcast(FP8X4),
+                scales=en2_scales[g][:, cols],
+                in_=en2[g][:, PACK * cols.start : PACK * cols.stop],
+            )
+
+        def second_product(g, branch, head, cols):
+            nc.tensor.matmul_mx(
+                out=head,
+                lhsT=head_codes[:, OUTS * branch : OUTS * (branch + 1)].bitcast(FP8X4),
+                lhsT_scale=head_scales[:, OUTS * branch : OUTS * (branch + 1)],
+                rhs=en2_codes[g][:, cols].bitcast(FP8X4),
+                rhs_scale=en2_scales[g][:, cols],
+                start=True,
+                stop=True,
+            )
 
         def second_products(g, tag):
-            pair = []
-            for branch in range(2):
-                head = psum.tile([P, CHUNK], F32, tag=tag)
-                nc.tensor.matmul_mx(
-                    out=head[:],
-                    lhsT=head_codes[:, OUTS * branch : OUTS * (branch + 1)].bitcast(FP8X4),
-                    lhsT_scale=head_scales[:, OUTS * branch : OUTS * (branch + 1)],
-                    rhs=en2_codes[g][:].bitcast(FP8X4),
-                    rhs_scale=en2_scales[g][:],
-                    start=True,
-                    stop=True,
-                )
-                pair.append(head)
-            heads[g] = pair
+            bank_v = psum.tile([P, CHUNK], F32, tag=tag)
+            second_product(g, VAR, bank_v[:], slice(0, CHUNK))
+            bank_m = psum.tile([P, CHUNK], F32, tag=tag)
+            second_product(g, MEAN, bank_m[:], slice(0, CHUNK))
+            heads[g] = (bank_m[:], bank_v[:])
 
-        stats = keep.tile([P, 2, CHUNKS, 6], F32)
+        def second_products_of_half(g, half):
+            bank = psum.tile([P, CHUNK], F32, tag="bank")
+            cols = slice(HALF * half, HALF * (half + 1))
+            second_product(g, VAR, bank[:, HALF:CHUNK], cols)
+            second_product(g, MEAN, bank[:, 0:HALF], cols)
+            heads[(g, half)] = (bank[:, 0:HALF], bank[:, HALF:CHUNK])
 
-        def statistics(g):
-            for branch in range(2):
-                nc.vector.bn_stats(out=stats[:, branch, g, :], in_=heads[g][branch][:])
+        stats = keep.tile([P, 2, CHUNKS + 1, 6], F32)
 
-        for g in range(CHUNKS):
+        def statistics(piece, branch, entry):
+            nc.vector.bn_stats(out=stats[:, branch, entry, :], in_=heads[piece][branch])
+
+        for g in range(LAST):
             if g >= FIRST_BATCH:
                 logarithm(g)
             quantise_en2(g)
-            second_products(g, "bank")
+            second_products(g, "acc" if g >= LAST - KEPT else "bank")
             if g > 0:
-                statistics(g - 1)
-        statistics(CHUNKS - 1)
+                statistics(g - 1, VAR, g - 1)
+                statistics(g - 1, MEAN, g - 1)
+        for half in range(2):
+            logarithm(LAST, half)
+            quantise_en2(LAST, half)
+            second_products_of_half(LAST, half)
+            if half == 0:
+                statistics(LAST - 1, VAR, LAST - 1)
         nc.scalar.activation(out=warm[:], in_=one[:], func=ACT.Exp)
 
-        for g in range(AHEAD):
-            second_products(g, "acc")
         moments = keep.tile([P, 2, 2], F32)
-        for branch in range(2):
-            nc.vector.bn_aggr(out=moments[:, branch, :], in_=stats[:, branch, :, :].rearrange("p g s -> p (g s)"))
         spread = keep.tile([P, 2], F32)
-        nc.gpsimd.tensor_scalar(
-            out=spread[:], in0=moments[:, :, 1], scalar1=1.0, scalar2=BN_EPS, op0=ALU.mult, op1=ALU.add
-        )
         rstd = keep.tile([P, 2], F32)
-        nc.gpsimd.tensor_tensor(out=rstd[:], in0=spread[:], in1=neg_half[:], op=ALU.pow)
-        scale = keep.tile([P, 2], F32)
-        nc.gpsimd.tensor_tensor(out=scale[:], in0=rstd[:], in1=gain[:], op=ALU.mult)
         centre = keep.tile([P, 2], F32)
-        nc.gpsimd.tensor_tensor(out=centre[:], in0=moments[:, :, 0], in1=scale[:], op=ALU.mult)
+        scale = keep.tile([P, 2], F32)
         offset = keep.tile([P, 2], F32)
-        nc.gpsimd.tensor_tensor(out=offset[:], in0=shift[:], in1=centre[:], op=ALU.subtract)
 
-        for g in range(CHUNKS):
-            mean_t = tail_pool.tile([P, CHUNK], F32)
-            nc.scalar.activation(
-                out=mean_t[:], in_=heads[g][0][:], func=ACT.Identity, scale=scale[:, 0:1], bias=offset[:, 0:1]
+        def finish_statistics(branch):
+            col = slice(branch, branch + 1)
+            nc.vector.bn_aggr(out=moments[:, branch, :], in_=stats[:, branch, :, :].rearrange("p g s -> p (g s)"))
+            nc.vector.tensor_scalar(
+                out=spread[:, col], in0=moments[:, branch, 1:2], scalar1=1.0, scalar2=BN_EPS, op0=ALU.mult, op1=ALU.add
             )
+            nc.gpsimd.tensor_tensor(out=rstd[:, col], in0=spread[:, col], in1=neg_half[:, col], op=ALU.pow)
+            nc.vector.tensor_tensor(
+                out=centre[:, col], in0=moments[:, branch, 0:1], in1=neg_gain[:, col], op=ALU.mult
+            )
+
+        def scale_and_offset(branch):
+            col = slice(branch, branch + 1)
+            nc.vector.tensor_tensor(out=scale[:, col], in0=rstd[:, col], in1=gain[:, col], op=ALU.mult)
+            nc.vector.scalar_tensor_tensor(
+                out=offset[:, col],
+                in0=centre[:, col],
+                scalar=rstd[:, col],
+                in1=shift[:, col],
+                op0=ALU.mult,
+                op1=ALU.add,
+            )
+
+        for half in range(2):
+            statistics((LAST, half), VAR, LAST + half)
+        finish_statistics(VAR)
+        statistics(LAST - 1, MEAN, LAST - 1)
+        for half in range(2):
+            statistics((LAST, half), MEAN, LAST + half)
+        scale_and_offset(VAR)
+        finish_statistics(MEAN)
+        scale_and_offset(MEAN)
+
+        pieces = [(LAST, 0), (LAST, 1)]
+        pieces += [(g, None) for g in range(LAST - KEPT, LAST)]
+        pieces += [(g, None) for g in range(LAST - KEPT - 1)]
+        pieces += [(LAST - KEPT - 1, 0), (LAST - KEPT - 1, 1)]
+        again = list(range(LAST - KEPT))
+
+        def head_of(piece, branch):
+            g, half = piece
+            if half is None:
+                return heads[g][branch]
+            if (g, half) in heads:
+                return heads[(g, half)][branch]
+            return heads[g][branch][:, HALF * half : HALF * (half + 1)]
+
+        def width_of(piece):
+            return CHUNK if piece[1] is None else HALF
+
+        def columns(piece):
+            g, half = piece
+            return slice(0, CHUNK) if half is None else slice(HALF * half, HALF * (half + 1))
+
+        def turn(piece, source):
+            bank = psum.tile([P, CHUNK], F32, tag="bank")
+            for j in range(width_of(piece) // P):
+                nc.tensor.transpose(bank[:, P * j : P * (j + 1)], source[:, P * j : P * (j + 1)], ident[:])
+            return bank
+
+        mean_banks = {}
+        noises = {}
+
+        def finish(piece):
+            width = width_of(piece)
+            z = tail_pool.tile([P, CHUNK], F32)
+            nc.vector.tensor_tensor(
+                out=z[:, 0:width], in0=mean_banks[piece][:, 0:width], in1=noises[piece][:, 0:width], op=ALU.add
+            )
+            nc.sync.dma_start(out=out_chunks[piece[0]][:, columns(piece)], in_=z[:, 0:width])
+
+        for i, piece in enumerate(pieces):
+            width = width_of(piece)
             dev_t = tail_pool.tile([P, CHUNK], F32)
             nc.scalar.activation(
-                out=dev_t[:], in_=heads[g][1][:], func=ACT.Exp, scale=scale[:, 1:2], bias=offset[:, 1:2]
+                out=dev_t[:, 0:width], in_=head_of(piece, VAR), func=ACT.Exp, scale=scale[:, 1:2], bias=offset[:, 1:2]
             )
-            if g + AHEAD < CHUNKS:
-                second_products(g + AHEAD, "acc")
-            mean_bank = psum.tile([P, CHUNK], F32, tag="bank")
-            dev_bank = psum.tile([P, CHUNK], F32, tag="bank")
-            for j in range(SUB):
-                nc.tensor.transpose(mean_bank[:, P * j : P * (j + 1)], mean_t[:, P * j : P * (j + 1)], ident[:])
-            for j in range(SUB):
-                nc.tensor.transpose(dev_bank[:, P * j : P * (j + 1)], dev_t[:, P * j : P * (j + 1)], ident[:])
+            mean_t = tail_pool.tile([P, CHUNK], F32)
+            nc.scalar.activation(
+                out=mean_t[:, 0:width], in_=head_of(piece, MEAN), func=ACT.Identity, scale=scale[:, 0:1], bias=offset[:, 0:1]
+            )
+            dev_bank = turn(piece, dev_t)
+            mean_bank = turn(piece, mean_t)
+            mean_banks[piece] = mean_bank
+            if i >= 2 and again:
+                second_products(again.pop(0), "acc")
             noise = tail_pool.tile([P, CHUNK], F32)
-            nc.vector.tensor_tensor(out=noise[:], in0=dev_bank[:], in1=eps_rows[:, g, :], op=ALU.mult)
-            z = tail_pool.tile([P, CHUNK], F32)
-            nc.vector.tensor_tensor(out=z[:], in0=mean_bank[:], in1=noise[:], op=ALU.add)
-            nc.sync.dma_start(out=out_chunks[g], in_=z[:])
+            nc.vector.tensor_tensor(
+                out=noise[:, 0:width],
+                in0=dev_bank[:, 0:width],
+                in1=eps_rows[:, piece[0], columns(piece)],
+                op=ALU.mult,
+            )
+            noises[piece] = noise
+            if i > 0:
+                finish(pieces[i - 1])
+        finish(pieces[-1])

@@ -23,7 +23,8 @@ ROW_WORDS = K1 // 2
 BN_EPS = 1e-5
 
 FIRST_BATCH = 3
-SPINS_AT_START = 6
+SPINS_AT_START = 5
+SPINS_AT_NORM = 4
 RAW_BUFS = 3
 LAST = CHUNKS - 1
 KEPT = 2
@@ -48,6 +49,7 @@ def tile_model_pa_t_kernel(tc, en1, eps, W2, b2, Wm, Wv, gm, betam, gv, betav, o
         exp_pool = ctx.enter_context(tc.tile_pool(name="exp", bufs=max(FIRST_BATCH, CHUNKS - FIRST_BATCH)))
         en2_pool = ctx.enter_context(tc.tile_pool(name="en2", bufs=FIRST_BATCH + 3))
         en2_codes_pool = ctx.enter_context(tc.tile_pool(name="en2codes", bufs=CHUNKS))
+        stash_pool = ctx.enter_context(tc.tile_pool(name="stash", bufs=FIRST_BATCH))
         tail_pool = ctx.enter_context(tc.tile_pool(name="tail", bufs=3))
         psum = ctx.enter_context(tc.psum_pool(name="psum", bufs=4))
 
@@ -93,13 +95,11 @@ def tile_model_pa_t_kernel(tc, en1, eps, W2, b2, Wm, Wv, gm, betam, gv, betav, o
 
         zeros = keep.tile([P, CHUNK], BF16)
         nc.vector.memset(zeros[:], 0.0)
-        unread = psum.tile([P, CHUNK], F32, tag="acc")
 
-        def spin(count):
+        def spin(bank, count):
             for i in range(count):
-                nc.tensor.matmul(out=unread[:], lhsT=zeros[:, 0:P], rhs=zeros[:], start=True, stop=True)
+                nc.tensor.matmul(out=bank[:], lhsT=zeros[:, 0:P], rhs=zeros[:], start=True, stop=True)
 
-        spin(SPINS_AT_START)
 
         one = keep.tile([P, 1], F32)
         nc.vector.memset(one[:], 1.0)
@@ -121,9 +121,10 @@ def tile_model_pa_t_kernel(tc, en1, eps, W2, b2, Wm, Wv, gm, betam, gv, betav, o
         nc.gpsimd.tensor_copy(out=shift[:, 0:1], in_=betam_raw[:])
         nc.gpsimd.tensor_scalar(out=shift[:, 1:2], in0=betav_raw[:], scalar1=0.5, scalar2=0.0, op0=ALU.mult, op1=ALU.add)
 
-        def transpose_slab(m):
+        def transpose_slab(m, spins=0):
             words = w2_raw[m][:].bitcast(F32)
             bank = psum.tile([P, CHUNK], F32, tag="bank")
+            spin(bank, spins)
             for plane in range(2 * PASSES):
                 nc.tensor.transpose(
                     bank[:, P * plane : P * (plane + 1)], words[:, P * plane : P * (plane + 1)], ident[:]
@@ -149,10 +150,12 @@ def tile_model_pa_t_kernel(tc, en1, eps, W2, b2, Wm, Wv, gm, betam, gv, betav, o
             w2_codes[m] = slab_codes
             w2_scales[m] = slab_scales
 
-        def transpose_half(g, h):
+        def transpose_half(g, h, spins):
             words = raw[(g, h)][:].bitcast(F32)
             for c in range(PASSES):
                 bank = psum.tile([P, CHUNK], F32, tag="bank")
+                if c == 0:
+                    spin(bank, spins)
                 for jj in range(2):
                     for u in range(2):
                         first = ROW_WORDS * jj + 2 * P * c + P * u
@@ -184,49 +187,44 @@ def tile_model_pa_t_kernel(tc, en1, eps, W2, b2, Wm, Wv, gm, betam, gv, betav, o
                 in_=grouped[(g, c, h)][:],
             )
 
-        def front(g):
-            for h in range(2):
-                transpose_half(g, h)
-            if g + RAW_BUFS < CHUNKS:
+        def front(g, h, spins=0):
+            transpose_half(g, h, spins)
+            if h == 1 and g + RAW_BUFS < CHUNKS:
                 load_chunk(g + RAW_BUFS)
-            for h in range(2):
-                for c in range(PASSES):
-                    copy_bank(nc.scalar.copy if c == 1 and g < FIRST_BATCH else nc.vector.tensor_copy, g, c, h)
-            open_codes(g)
-            for h in range(2):
-                for c in range(PASSES):
-                    quantise_bank(g, c, h)
+            for c in range(PASSES):
+                copy_bank(nc.scalar.copy if c == 1 and g < FIRST_BATCH else nc.vector.tensor_copy, g, c, h)
+            if h == 0:
+                open_codes(g)
+            for c in range(PASSES):
+                quantise_bank(g, c, h)
 
-        transpose_slab(0)
+        transpose_slab(0, SPINS_AT_START)
         copy_slab(0)
         quantise_slab(0)
-        front(0)
+        front(0, 0)
+        front(0, 1, spins=1)
         for m in range(1, PACK):
-            transpose_slab(m)
+            transpose_slab(m, spins=1 if m == 1 else 0)
             copy_slab(m)
         for m in range(1, PACK):
             quantise_slab(m)
 
-        def first_product(g):
-            for m in range(PACK):
-                acc = psum.tile([P, CHUNK], F32, tag="acc")
-                for c in range(PASSES):
-                    nc.tensor.matmul_mx(
-                        out=acc[:],
-                        lhsT=w2_codes[m][:, c, :].bitcast(FP8X4),
-                        lhsT_scale=w2_scales[m][:, c, :],
-                        rhs=codes[g][:, c, :].bitcast(FP8X4),
-                        rhs_scale=scales[g][:, c, :],
-                        start=(c == 0),
-                        stop=(c == PASSES - 1),
-                    )
-                sums[(g, m)] = acc
-
-        def exponentials(g):
-            e = exp_pool.tile([P, PACK, CHUNK], F32)
-            for m in range(PACK):
-                nc.scalar.activation(out=e[:, m, :], in_=sums[(g, m)][:], func=ACT.Exp, bias=b2_f32[:, m : m + 1])
-            expo[g] = e
+        def bank_of_product(g, m):
+            acc = psum.tile([P, CHUNK], F32, tag="acc")
+            for c in range(PASSES):
+                nc.tensor.matmul_mx(
+                    out=acc[:],
+                    lhsT=w2_codes[m][:, c, :].bitcast(FP8X4),
+                    lhsT_scale=w2_scales[m][:, c, :],
+                    rhs=codes[g][:, c, :].bitcast(FP8X4),
+                    rhs_scale=scales[g][:, c, :],
+                    start=(c == 0),
+                    stop=(c == PASSES - 1),
+                )
+            if m == 0:
+                e = exp_pool.tile([P, PACK, CHUNK], F32)
+                expo[g] = e
+            nc.scalar.activation(out=expo[g][:, m, :], in_=acc[:], func=ACT.Exp, bias=b2_f32[:, m : m + 1])
 
         def logarithm(g, half=None):
             if half in (None, 0):
@@ -240,15 +238,29 @@ def tile_model_pa_t_kernel(tc, en1, eps, W2, b2, Wm, Wv, gm, betam, gv, betav, o
                 bias=one[:],
             )
 
-        fronts = {0: (1, 2), FIRST_BATCH - 1: (3, 4), FIRST_BATCH: (5, 6, 7)}
-        for g in range(CHUNKS):
-            first_product(g)
-            exponentials(g)
-            for ahead in fronts.get(g, ()):
-                front(ahead)
-            if g == FIRST_BATCH - 1:
-                for q in range(FIRST_BATCH):
-                    logarithm(q)
+        for m in range(PACK):
+            bank_of_product(0, m)
+            front(1 + m // 2, m % 2)
+        for m in range(PACK):
+            bank_of_product(1, m)
+        front(3, 0)
+        for m in range(PACK):
+            bank_of_product(2, m)
+        for q in range(FIRST_BATCH):
+            logarithm(q)
+        front(3, 1, spins=1)
+        front(4, 0, spins=1)
+        front(4, 1, spins=1)
+        for m, (g, h) in enumerate(((5, 0), (5, 1), (6, 0), (6, 1))):
+            bank_of_product(3, m)
+            front(g, h, spins=1)
+        for m in range(PACK):
+            bank_of_product(4, m)
+            if m == 1:
+                front(7, 0)
+        for m in range(PACK):
+            bank_of_product(5, m)
+        front(7, 1)
 
         wm_raw = keep.tile([P, HIDDEN], BF16)
         nc.sync.dma_start(out=wm_raw[:], in_=Wm)
@@ -272,6 +284,10 @@ def tile_model_pa_t_kernel(tc, en1, eps, W2, b2, Wm, Wv, gm, betam, gv, betav, o
         head_codes = keep.tile([P, 2 * OUTS], U32, align_bytes=64)
         head_scales = keep.tile([P, 2 * OUTS], U8, align_bytes=64)
         nc.vector.quantize_mx(out=head_codes[:].bitcast(FP8X4), scales=head_scales[:], in_=head_grouped[:])
+
+        for g in range(FIRST_BATCH + 3, CHUNKS):
+            for m in range(PACK):
+                bank_of_product(g, m)
 
         en2_codes = {}
         en2_scales = {}
@@ -300,8 +316,9 @@ def tile_model_pa_t_kernel(tc, en1, eps, W2, b2, Wm, Wv, gm, betam, gv, betav, o
                 stop=True,
             )
 
-        def second_products(g, tag):
+        def second_products(g, tag, spins=0):
             bank_v = psum.tile([P, CHUNK], F32, tag=tag)
+            spin(bank_v, spins)
             second_product(g, VAR, bank_v[:], slice(0, CHUNK))
             bank_m = psum.tile([P, CHUNK], F32, tag=tag)
             second_product(g, MEAN, bank_m[:], slice(0, CHUNK))
@@ -319,20 +336,46 @@ def tile_model_pa_t_kernel(tc, en1, eps, W2, b2, Wm, Wv, gm, betam, gv, betav, o
         def statistics(piece, branch, entry):
             nc.vector.bn_stats(out=stats[:, branch, entry, :], in_=heads[piece][branch])
 
-        for g in range(LAST):
-            if g >= FIRST_BATCH:
-                logarithm(g)
+        def statistics_of_chunk(g):
+            statistics(g, VAR, g)
+            statistics(g, MEAN, g)
+
+        def stash(g):
+            kept = stash_pool.tile([P, 2, CHUNK], F32)
+            for branch in range(2):
+                nc.vector.tensor_copy(out=kept[:, branch, :], in_=heads[g][branch])
+            heads[g] = (kept[:, MEAN, :], kept[:, VAR, :])
+
+        for g in range(FIRST_BATCH):
             quantise_en2(g)
-            second_products(g, "acc" if g >= LAST - KEPT else "bank")
+        for g in range(FIRST_BATCH):
+            second_products(g, "bank")
             if g > 0:
+                statistics_of_chunk(g - 1)
+                stash(g - 1)
+        statistics_of_chunk(FIRST_BATCH - 1)
+        for g in range(FIRST_BATCH, LAST):
+            logarithm(g)
+            quantise_en2(g)
+            second_products(g, "acc" if g >= LAST - KEPT else "bank", spins=1)
+            if g == FIRST_BATCH:
+                stash(g - 1)
+            elif g < LAST - 1:
+                statistics_of_chunk(g - 1)
+            else:
                 statistics(g - 1, VAR, g - 1)
-                statistics(g - 1, MEAN, g - 1)
-        for half in range(2):
-            logarithm(LAST, half)
-            quantise_en2(LAST, half)
-            second_products_of_half(LAST, half)
-            if half == 0:
-                statistics(LAST - 1, VAR, LAST - 1)
+        statistics(LAST - 2, MEAN, LAST - 2)
+        logarithm(LAST, 0)
+        quantise_en2(LAST, 0)
+        second_products_of_half(LAST, 0)
+        statistics(LAST - 1, VAR, LAST - 1)
+        statistics((LAST, 0), VAR, LAST)
+        logarithm(LAST, 1)
+        quantise_en2(LAST, 1)
+        second_products_of_half(LAST, 1)
+        statistics(LAST - 1, MEAN, LAST - 1)
+        first_dev_bank = psum.tile([P, CHUNK], F32, tag="bank")
+        spin(first_dev_bank, SPINS_AT_NORM)
         nc.scalar.activation(out=warm[:], in_=one[:], func=ACT.Exp)
 
         moments = keep.tile([P, 2, 2], F32)
@@ -365,10 +408,8 @@ def tile_model_pa_t_kernel(tc, en1, eps, W2, b2, Wm, Wv, gm, betam, gv, betav, o
                 op1=ALU.add,
             )
 
-        for half in range(2):
-            statistics((LAST, half), VAR, LAST + half)
+        statistics((LAST, 1), VAR, LAST + 1)
         finish_statistics(VAR)
-        statistics(LAST - 1, MEAN, LAST - 1)
         for half in range(2):
             statistics((LAST, half), MEAN, LAST + half)
         scale_and_offset(VAR)
@@ -379,7 +420,7 @@ def tile_model_pa_t_kernel(tc, en1, eps, W2, b2, Wm, Wv, gm, betam, gv, betav, o
         pieces += [(g, None) for g in range(LAST - KEPT, LAST)]
         pieces += [(g, None) for g in range(LAST - KEPT - 1)]
         pieces += [(LAST - KEPT - 1, 0), (LAST - KEPT - 1, 1)]
-        again = list(range(LAST - KEPT))
+        again = list(range(FIRST_BATCH, LAST - KEPT))
 
         def head_of(piece, branch):
             g, half = piece
@@ -396,46 +437,74 @@ def tile_model_pa_t_kernel(tc, en1, eps, W2, b2, Wm, Wv, gm, betam, gv, betav, o
             g, half = piece
             return slice(0, CHUNK) if half is None else slice(HALF * half, HALF * (half + 1))
 
-        def turn(piece, source):
-            bank = psum.tile([P, CHUNK], F32, tag="bank")
+        def turn(piece, source, bank):
             for j in range(width_of(piece) // P):
                 nc.tensor.transpose(bank[:, P * j : P * (j + 1)], source[:, P * j : P * (j + 1)], ident[:])
-            return bank
 
+        devs = {}
+        means = {}
         mean_banks = {}
-        noises = {}
 
-        def finish(piece):
-            width = width_of(piece)
-            z = tail_pool.tile([P, CHUNK], F32)
-            nc.vector.tensor_tensor(
-                out=z[:, 0:width], in0=mean_banks[piece][:, 0:width], in1=noises[piece][:, 0:width], op=ALU.add
-            )
-            nc.sync.dma_start(out=out_chunks[piece[0]][:, columns(piece)], in_=z[:, 0:width])
-
-        for i, piece in enumerate(pieces):
+        def deviation(piece):
             width = width_of(piece)
             dev_t = tail_pool.tile([P, CHUNK], F32)
             nc.scalar.activation(
                 out=dev_t[:, 0:width], in_=head_of(piece, VAR), func=ACT.Exp, scale=scale[:, 1:2], bias=offset[:, 1:2]
             )
+            devs[piece] = dev_t
+
+        def mean(piece):
+            width = width_of(piece)
             mean_t = tail_pool.tile([P, CHUNK], F32)
             nc.scalar.activation(
                 out=mean_t[:, 0:width], in_=head_of(piece, MEAN), func=ACT.Identity, scale=scale[:, 0:1], bias=offset[:, 0:1]
             )
-            dev_bank = turn(piece, dev_t)
-            mean_bank = turn(piece, mean_t)
+            means[piece] = mean_t
+
+        def turn_mean(piece):
+            mean_bank = psum.tile([P, CHUNK], F32, tag="bank")
+            turn(piece, means[piece], mean_bank)
             mean_banks[piece] = mean_bank
-            if i >= 2 and again:
-                second_products(again.pop(0), "acc")
+
+        def finish(piece, dev_bank):
+            width = width_of(piece)
             noise = tail_pool.tile([P, CHUNK], F32)
-            nc.vector.tensor_tensor(
-                out=noise[:, 0:width],
-                in0=dev_bank[:, 0:width],
-                in1=eps_rows[:, piece[0], columns(piece)],
-                op=ALU.mult,
-            )
-            noises[piece] = noise
+            z = tail_pool.tile([P, CHUNK], F32)
+            first = columns(piece).start
+            parts = [slice(width // 2 * part, width // 2 * (part + 1)) for part in range(2)]
+            for cols in parts:
+                nc.vector.tensor_tensor(
+                    out=noise[:, cols],
+                    in0=dev_bank[:, cols],
+                    in1=eps_rows[:, piece[0], first + cols.start : first + cols.stop],
+                    op=ALU.mult,
+                )
+            for cols in parts:
+                nc.vector.tensor_tensor(
+                    out=z[:, cols], in0=mean_banks[piece][:, cols], in1=noise[:, cols], op=ALU.add
+                )
+            nc.sync.dma_start(out=out_chunks[piece[0]][:, columns(piece)], in_=z[:, 0:width])
+
+        for piece in pieces[0:3]:
+            deviation(piece)
+        second_dev_bank = psum.tile([P, CHUNK], F32, tag="bank")
+        for piece, dev_bank in zip(pieces[0:2], (first_dev_bank, second_dev_bank)):
+            turn(piece, devs[piece], dev_bank)
+        for piece in pieces[0:2]:
+            mean(piece)
+            turn_mean(piece)
+        for piece, dev_bank in zip(pieces[0:2], (first_dev_bank, second_dev_bank)):
+            finish(piece, dev_bank)
+
+        for i, piece in enumerate(pieces[2:]):
             if i > 0:
-                finish(pieces[i - 1])
-        finish(pieces[-1])
+                deviation(piece)
+            mean(piece)
+            dev_bank = psum.tile([P, CHUNK], F32, tag="bank")
+            if piece[0] in range(FIRST_BATCH + 1):
+                spin(dev_bank, 1)
+            turn(piece, devs[piece], dev_bank)
+            turn_mean(piece)
+            if again:
+                second_products(again.pop(0), "acc")
+            finish(piece, dev_bank)

@@ -198,13 +198,13 @@ def tile_model_pa_t_kernel(tc, en1, eps, W2, b2, Wm, Wv, gm, betam, gv, betav, o
             for c in range(PASSES):
                 quantise_bank(g, c, h)
 
-        transpose_slab(0, SPINS_AT_START)
+        transpose_slab(0, 5)
         copy_slab(0)
         quantise_slab(0)
-        front(0, 0)
+        front(0, 0, spins=1)
         front(0, 1, spins=1)
         for m in range(1, PACK):
-            transpose_slab(m, spins=1 if m == 1 else 0)
+            transpose_slab(m, spins=(0, 1, 0, 0)[m])
             copy_slab(m)
         for m in range(1, PACK):
             quantise_slab(m)
@@ -238,57 +238,35 @@ def tile_model_pa_t_kernel(tc, en1, eps, W2, b2, Wm, Wv, gm, betam, gv, betav, o
                 bias=one[:],
             )
 
-        for m in range(PACK):
-            bank_of_product(0, m)
-            front(1 + m // 2, m % 2)
-        for m in range(PACK):
-            bank_of_product(1, m)
-        front(3, 0)
-        for m in range(PACK):
-            bank_of_product(2, m)
-        for q in range(FIRST_BATCH):
-            logarithm(q)
-        front(3, 1, spins=1)
-        front(4, 0, spins=1)
-        front(4, 1, spins=1)
-        for m, (g, h) in enumerate(((5, 0), (5, 1), (6, 0), (6, 1))):
-            bank_of_product(3, m)
-            front(g, h, spins=1)
-        for m in range(PACK):
-            bank_of_product(4, m)
-            if m == 1:
-                front(7, 0)
-        for m in range(PACK):
-            bank_of_product(5, m)
-        front(7, 1)
+        hp = {}
+        def head_prep():
+            wm_raw = keep.tile([P, HIDDEN], BF16)
+            nc.sync.dma_start(out=wm_raw[:], in_=Wm)
+            wv_raw = keep.tile([P, HIDDEN], BF16)
+            nc.sync.dma_start(out=wv_raw[:], in_=Wv)
+            eps_rows = keep.tile([P, CHUNKS, CHUNK], BF16)
+            nc.sync.dma_start(out=eps_rows[:], in_=eps_chunks)
 
-        wm_raw = keep.tile([P, HIDDEN], BF16)
-        nc.sync.dma_start(out=wm_raw[:], in_=Wm)
-        wv_raw = keep.tile([P, HIDDEN], BF16)
-        nc.sync.dma_start(out=wv_raw[:], in_=Wv)
-        eps_rows = keep.tile([P, CHUNKS, CHUNK], BF16)
-        nc.sync.dma_start(out=eps_rows[:], in_=eps_chunks)
+            head_bank = psum.tile([P, CHUNK], F32, tag="bank")
+            for branch, head_raw in enumerate((wm_raw, wv_raw)):
+                planes = head_raw[:].bitcast(F32).rearrange("p (q u) -> p u q", u=2)
+                for u in range(2):
+                    nc.tensor.transpose(
+                        head_bank[:, HALF * u + P * branch : HALF * u + P * (branch + 1)], planes[:, u, :], ident[:]
+                    )
+            head_grouped = keep.tile([P, 2 * OUTS * PACK], BF16, align_bytes=64)
+            nc.vector.tensor_copy(
+                out=head_grouped[:].bitcast(F32).rearrange("p (r u) -> p r u", u=2),
+                in_=head_bank[:].rearrange("p (u r) -> p r u", u=2),
+            )
+            head_codes = keep.tile([P, 2 * OUTS], U32, align_bytes=64)
+            head_scales = keep.tile([P, 2 * OUTS], U8, align_bytes=64)
+            nc.vector.quantize_mx(out=head_codes[:].bitcast(FP8X4), scales=head_scales[:], in_=head_grouped[:])
 
-        head_bank = psum.tile([P, CHUNK], F32, tag="bank")
-        for branch, head_raw in enumerate((wm_raw, wv_raw)):
-            planes = head_raw[:].bitcast(F32).rearrange("p (q u) -> p u q", u=2)
-            for u in range(2):
-                nc.tensor.transpose(
-                    head_bank[:, HALF * u + P * branch : HALF * u + P * (branch + 1)], planes[:, u, :], ident[:]
-                )
-        head_grouped = keep.tile([P, 2 * OUTS * PACK], BF16, align_bytes=64)
-        nc.vector.tensor_copy(
-            out=head_grouped[:].bitcast(F32).rearrange("p (r u) -> p r u", u=2),
-            in_=head_bank[:].rearrange("p (u r) -> p r u", u=2),
-        )
-        head_codes = keep.tile([P, 2 * OUTS], U32, align_bytes=64)
-        head_scales = keep.tile([P, 2 * OUTS], U8, align_bytes=64)
-        nc.vector.quantize_mx(out=head_codes[:].bitcast(FP8X4), scales=head_scales[:], in_=head_grouped[:])
 
-        for g in range(FIRST_BATCH + 3, CHUNKS):
-            for m in range(PACK):
-                bank_of_product(g, m)
-
+            hp["eps"] = eps_rows
+            hp["codes"] = head_codes
+            hp["scales"] = head_scales
         en2_codes = {}
         en2_scales = {}
 
@@ -308,8 +286,8 @@ def tile_model_pa_t_kernel(tc, en1, eps, W2, b2, Wm, Wv, gm, betam, gv, betav, o
         def second_product(g, branch, head, cols):
             nc.tensor.matmul_mx(
                 out=head,
-                lhsT=head_codes[:, OUTS * branch : OUTS * (branch + 1)].bitcast(FP8X4),
-                lhsT_scale=head_scales[:, OUTS * branch : OUTS * (branch + 1)],
+                lhsT=hp["codes"][:, OUTS * branch : OUTS * (branch + 1)].bitcast(FP8X4),
+                lhsT_scale=hp["scales"][:, OUTS * branch : OUTS * (branch + 1)],
                 rhs=en2_codes[g][:, cols].bitcast(FP8X4),
                 rhs_scale=en2_scales[g][:, cols],
                 start=True,
@@ -346,36 +324,71 @@ def tile_model_pa_t_kernel(tc, en1, eps, W2, b2, Wm, Wv, gm, betam, gv, betav, o
                 nc.vector.tensor_copy(out=kept[:, branch, :], in_=heads[g][branch])
             heads[g] = (kept[:, MEAN, :], kept[:, VAR, :])
 
+
+        def banks_of_chunk(g):
+            for m in range(PACK):
+                bank_of_product(g, m)
+
+        def front_of_chunk(g):
+            for h in range(2):
+                front(g, h)
+
+        for m in range(2):
+            bank_of_product(0, m)
+        front_of_chunk(1)
+        for m in range(2, PACK):
+            bank_of_product(0, m)
+        front_of_chunk(2)
+        banks_of_chunk(1)
+        banks_of_chunk(2)
+        for g in range(FIRST_BATCH):
+            logarithm(g)
+        front_of_chunk(3)
+        front_of_chunk(4)
+        bank_of_product(3, 0)
+        bank_of_product(3, 1)
+        front(5, 0)
+        bank_of_product(3, 2)
+        front(5, 1)
+        bank_of_product(3, 3)
+        for h in range(2):
+            front(6, h, spins=2)
+        banks_of_chunk(4)
+        front_of_chunk(7)
+        banks_of_chunk(5)
+        head_prep()
+        banks_of_chunk(6)
+        banks_of_chunk(7)
+
         for g in range(FIRST_BATCH):
             quantise_en2(g)
-        for g in range(FIRST_BATCH):
+        for g in range(2):
             second_products(g, "bank")
-            if g > 0:
-                statistics_of_chunk(g - 1)
-                stash(g - 1)
-        statistics_of_chunk(FIRST_BATCH - 1)
+        for g in range(2):
+            statistics_of_chunk(g)
+            stash(g)
+            if g == 0:
+                second_products(2, "bank")
         for g in range(FIRST_BATCH, LAST):
             logarithm(g)
             quantise_en2(g)
             second_products(g, "acc" if g >= LAST - KEPT else "bank", spins=1)
+            if g < LAST - 1:
+                statistics_of_chunk(g - 1)
             if g == FIRST_BATCH:
                 stash(g - 1)
-            elif g < LAST - 1:
-                statistics_of_chunk(g - 1)
-            else:
-                statistics(g - 1, VAR, g - 1)
-        statistics(LAST - 2, MEAN, LAST - 2)
+        statistics(LAST - 2, VAR, LAST - 2)
         logarithm(LAST, 0)
         quantise_en2(LAST, 0)
         second_products_of_half(LAST, 0)
-        statistics(LAST - 1, VAR, LAST - 1)
-        statistics((LAST, 0), VAR, LAST)
+        statistics(LAST - 2, MEAN, LAST - 2)
         logarithm(LAST, 1)
         quantise_en2(LAST, 1)
         second_products_of_half(LAST, 1)
-        statistics(LAST - 1, MEAN, LAST - 1)
+        statistics(LAST - 1, VAR, LAST - 1)
+        statistics((LAST, 0), VAR, LAST)
         first_dev_bank = psum.tile([P, CHUNK], F32, tag="bank")
-        spin(first_dev_bank, SPINS_AT_NORM)
+        spin(first_dev_bank, 2)
         nc.scalar.activation(out=warm[:], in_=one[:], func=ACT.Exp)
 
         moments = keep.tile([P, 2, 2], F32)
@@ -385,16 +398,15 @@ def tile_model_pa_t_kernel(tc, en1, eps, W2, b2, Wm, Wv, gm, betam, gv, betav, o
         scale = keep.tile([P, 2], F32)
         offset = keep.tile([P, 2], F32)
 
-        def finish_statistics(branch):
-            col = slice(branch, branch + 1)
+        def aggregate(branch):
             nc.vector.bn_aggr(out=moments[:, branch, :], in_=stats[:, branch, :, :].rearrange("p g s -> p (g s)"))
+
+        def power(branch):
+            col = slice(branch, branch + 1)
             nc.vector.tensor_scalar(
                 out=spread[:, col], in0=moments[:, branch, 1:2], scalar1=1.0, scalar2=BN_EPS, op0=ALU.mult, op1=ALU.add
             )
             nc.gpsimd.tensor_tensor(out=rstd[:, col], in0=spread[:, col], in1=neg_half[:, col], op=ALU.pow)
-            nc.vector.tensor_tensor(
-                out=centre[:, col], in0=moments[:, branch, 0:1], in1=neg_gain[:, col], op=ALU.mult
-            )
 
         def scale_and_offset(branch):
             col = slice(branch, branch + 1)
@@ -408,103 +420,108 @@ def tile_model_pa_t_kernel(tc, en1, eps, W2, b2, Wm, Wv, gm, betam, gv, betav, o
                 op1=ALU.add,
             )
 
+        def centre_of(branch):
+            col = slice(branch, branch + 1)
+            nc.vector.tensor_tensor(out=centre[:, col], in0=moments[:, branch, 0:1], in1=neg_gain[:, col], op=ALU.mult)
+
         statistics((LAST, 1), VAR, LAST + 1)
-        finish_statistics(VAR)
-        for half in range(2):
-            statistics((LAST, half), MEAN, LAST + half)
+        statistics((LAST, 0), MEAN, LAST)
+        aggregate(VAR)
+        statistics((LAST, 1), MEAN, LAST + 1)
+        power(VAR)
+        nc.vector.memset(zeros[:, 0:2], 0.0)
+        spin(first_dev_bank, 3)
+        centre_of(VAR)
+        statistics(LAST - 1, MEAN, LAST - 1)
+        aggregate(MEAN)
         scale_and_offset(VAR)
-        finish_statistics(MEAN)
+        power(MEAN)
+        centre_of(MEAN)
         scale_and_offset(MEAN)
 
-        pieces = [(LAST, 0), (LAST, 1)]
-        pieces += [(g, None) for g in range(LAST - KEPT, LAST)]
-        pieces += [(g, None) for g in range(LAST - KEPT - 1)]
-        pieces += [(LAST - KEPT - 1, 0), (LAST - KEPT - 1, 1)]
-        again = list(range(FIRST_BATCH, LAST - KEPT))
-
-        def head_of(piece, branch):
-            g, half = piece
-            if half is None:
-                return heads[g][branch]
-            if (g, half) in heads:
-                return heads[(g, half)][branch]
-            return heads[g][branch][:, HALF * half : HALF * (half + 1)]
-
-        def width_of(piece):
-            return CHUNK if piece[1] is None else HALF
-
-        def columns(piece):
-            g, half = piece
-            return slice(0, CHUNK) if half is None else slice(HALF * half, HALF * (half + 1))
-
-        def turn(piece, source, bank):
-            for j in range(width_of(piece) // P):
-                nc.tensor.transpose(bank[:, P * j : P * (j + 1)], source[:, P * j : P * (j + 1)], ident[:])
-
+        order = [7, 5, 6, 0, 3, 1, 4, 2]
+        again = {2: 3, 3: 4}
         devs = {}
         means = {}
+        dev_banks = {}
         mean_banks = {}
+        noises = {}
 
-        def deviation(piece):
-            width = width_of(piece)
+        def parts_of(g, branch):
+            if g == LAST:
+                return [(heads[(LAST, half)][branch], slice(HALF * half, HALF * (half + 1))) for half in range(2)]
+            return [(heads[g][branch], slice(0, CHUNK))]
+
+        def deviation(g):
             dev_t = tail_pool.tile([P, CHUNK], F32)
-            nc.scalar.activation(
-                out=dev_t[:, 0:width], in_=head_of(piece, VAR), func=ACT.Exp, scale=scale[:, 1:2], bias=offset[:, 1:2]
-            )
-            devs[piece] = dev_t
+            for head, cols in parts_of(g, VAR):
+                nc.scalar.activation(out=dev_t[:, cols], in_=head, func=ACT.Exp, scale=scale[:, 1:2], bias=offset[:, 1:2])
+            devs[g] = dev_t
 
-        def mean(piece):
-            width = width_of(piece)
+        def mean(g):
             mean_t = tail_pool.tile([P, CHUNK], F32)
-            nc.scalar.activation(
-                out=mean_t[:, 0:width], in_=head_of(piece, MEAN), func=ACT.Identity, scale=scale[:, 0:1], bias=offset[:, 0:1]
-            )
-            means[piece] = mean_t
+            for head, cols in parts_of(g, MEAN):
+                nc.scalar.activation(
+                    out=mean_t[:, cols], in_=head, func=ACT.Identity, scale=scale[:, 0:1], bias=offset[:, 0:1]
+                )
+            means[g] = mean_t
 
-        def turn_mean(piece):
-            mean_bank = psum.tile([P, CHUNK], F32, tag="bank")
-            turn(piece, means[piece], mean_bank)
-            mean_banks[piece] = mean_bank
+        def turn(source, bank):
+            for j in range(SUB):
+                nc.tensor.transpose(bank[:, P * j : P * (j + 1)], source[:, P * j : P * (j + 1)], ident[:])
 
-        def finish(piece, dev_bank):
-            width = width_of(piece)
+        def turn_deviation(g, spins):
+            bank = first_dev_bank
+            if g != LAST:
+                bank = psum.tile([P, CHUNK], F32, tag="bank")
+            spin(bank, spins)
+            turn(devs[g], bank)
+            dev_banks[g] = bank
+
+        def turn_mean(g):
+            bank = psum.tile([P, CHUNK], F32, tag="bank")
+            turn(means[g], bank)
+            mean_banks[g] = bank
+
+        halves = (slice(0, HALF), slice(HALF, CHUNK))
+
+        def multiply(g):
             noise = tail_pool.tile([P, CHUNK], F32)
+            for cols in halves:
+                nc.vector.tensor_tensor(
+                    out=noise[:, cols], in0=dev_banks[g][:, cols], in1=hp["eps"][:, g, cols], op=ALU.mult
+                )
+            noises[g] = noise
+
+        def add_and_store(g):
             z = tail_pool.tile([P, CHUNK], F32)
-            first = columns(piece).start
-            parts = [slice(width // 2 * part, width // 2 * (part + 1)) for part in range(2)]
-            for cols in parts:
-                nc.vector.tensor_tensor(
-                    out=noise[:, cols],
-                    in0=dev_bank[:, cols],
-                    in1=eps_rows[:, piece[0], first + cols.start : first + cols.stop],
-                    op=ALU.mult,
-                )
-            for cols in parts:
-                nc.vector.tensor_tensor(
-                    out=z[:, cols], in0=mean_banks[piece][:, cols], in1=noise[:, cols], op=ALU.add
-                )
-            nc.sync.dma_start(out=out_chunks[piece[0]][:, columns(piece)], in_=z[:, 0:width])
+            for cols in halves:
+                nc.vector.tensor_tensor(out=z[:, cols], in0=mean_banks[g][:, cols], in1=noises[g][:, cols], op=ALU.add)
+                if g == order[-1]:
+                    nc.sync.dma_start(out=out_chunks[g][:, cols], in_=z[:, cols])
+            if g != order[-1]:
+                nc.sync.dma_start(out=out_chunks[g], in_=z[:])
 
-        for piece in pieces[0:3]:
-            deviation(piece)
-        second_dev_bank = psum.tile([P, CHUNK], F32, tag="bank")
-        for piece, dev_bank in zip(pieces[0:2], (first_dev_bank, second_dev_bank)):
-            turn(piece, devs[piece], dev_bank)
-        for piece in pieces[0:2]:
-            mean(piece)
-            turn_mean(piece)
-        for piece, dev_bank in zip(pieces[0:2], (first_dev_bank, second_dev_bank)):
-            finish(piece, dev_bank)
-
-        for i, piece in enumerate(pieces[2:]):
-            if i > 0:
-                deviation(piece)
-            mean(piece)
-            dev_bank = psum.tile([P, CHUNK], F32, tag="bank")
-            if piece[0] in range(FIRST_BATCH + 1):
-                spin(dev_bank, 1)
-            turn(piece, devs[piece], dev_bank)
-            turn_mean(piece)
-            if again:
-                second_products(again.pop(0), "acc")
-            finish(piece, dev_bank)
+        a, b = order[0:2]
+        deviation(a)
+        deviation(b)
+        mean(a)
+        mean(b)
+        turn_deviation(a, 1)
+        turn_deviation(b, 1)
+        turn_mean(a)
+        turn_mean(b)
+        multiply(a)
+        multiply(b)
+        add_and_store(a)
+        add_and_store(b)
+        for i, g in enumerate(order):
+            if i in again:
+                second_products(again[i], "acc")
+            if i >= 2:
+                deviation(g)
+                mean(g)
+                turn_deviation(g, 1)
+                turn_mean(g)
+                multiply(g)
+                add_and_store(g)

@@ -49,6 +49,7 @@ def tile_model_pa_t_kernel(tc, en1, eps, W2, b2, Wm, Wv, gm, betam, gv, betav, o
         exp_pool = ctx.enter_context(tc.tile_pool(name="exp", bufs=max(FIRST_BATCH, CHUNKS - FIRST_BATCH)))
         en2_pool = ctx.enter_context(tc.tile_pool(name="en2", bufs=FIRST_BATCH + 3))
         en2_codes_pool = ctx.enter_context(tc.tile_pool(name="en2codes", bufs=CHUNKS))
+        z_pool = ctx.enter_context(tc.tile_pool(name="z", bufs=6))
         stash_pool = ctx.enter_context(tc.tile_pool(name="stash", bufs=FIRST_BATCH))
         tail_pool = ctx.enter_context(tc.tile_pool(name="tail", bufs=3))
         psum = ctx.enter_context(tc.psum_pool(name="psum", bufs=4))
@@ -351,12 +352,12 @@ def tile_model_pa_t_kernel(tc, en1, eps, W2, b2, Wm, Wv, gm, betam, gv, betav, o
         bank_of_product(3, 2)
         front(5, 1)
         bank_of_product(3, 3)
-        for h in range(2):
-            front(6, h, spins=2)
+        for g, h in ((6, 0), (6, 1), (7, 0)):
+            front(g, h, spins=2)
         banks_of_chunk(4)
-        front_of_chunk(7)
-        banks_of_chunk(5)
+        front(7, 1)
         head_prep()
+        banks_of_chunk(5)
         banks_of_chunk(6)
         banks_of_chunk(7)
 
@@ -440,7 +441,7 @@ def tile_model_pa_t_kernel(tc, en1, eps, W2, b2, Wm, Wv, gm, betam, gv, betav, o
         scale_and_offset(MEAN)
 
         order = [7, 5, 6, 0, 3, 1, 4, 2]
-        again = {2: 3, 3: 4}
+        again = {5: 3, 0: 4}
         devs = {}
         means = {}
         dev_banks = {}
@@ -470,18 +471,29 @@ def tile_model_pa_t_kernel(tc, en1, eps, W2, b2, Wm, Wv, gm, betam, gv, betav, o
             for j in range(SUB):
                 nc.tensor.transpose(bank[:, P * j : P * (j + 1)], source[:, P * j : P * (j + 1)], ident[:])
 
-        def turn_deviation(g, spins):
+        def turn_deviation(g):
             bank = first_dev_bank
             if g != LAST:
                 bank = psum.tile([P, CHUNK], F32, tag="bank")
-            spin(bank, spins)
             turn(devs[g], bank)
             dev_banks[g] = bank
+            if g in again:
+                again_product(again[g], VAR)
 
         def turn_mean(g):
             bank = psum.tile([P, CHUNK], F32, tag="bank")
             turn(means[g], bank)
             mean_banks[g] = bank
+            if g in again:
+                again_product(again[g], MEAN)
+
+        def again_product(g, branch):
+            bank = psum.tile([P, CHUNK], F32, tag="acc")
+            second_product(g, branch, bank[:], slice(0, CHUNK))
+            if branch == VAR:
+                heads[g] = (None, bank[:])
+            else:
+                heads[g] = (bank[:], heads[g][VAR])
 
         halves = (slice(0, HALF), slice(HALF, CHUNK))
 
@@ -494,7 +506,7 @@ def tile_model_pa_t_kernel(tc, en1, eps, W2, b2, Wm, Wv, gm, betam, gv, betav, o
             noises[g] = noise
 
         def add_and_store(g):
-            z = tail_pool.tile([P, CHUNK], F32)
+            z = z_pool.tile([P, CHUNK], F32)
             for cols in halves:
                 nc.vector.tensor_tensor(out=z[:, cols], in0=mean_banks[g][:, cols], in1=noises[g][:, cols], op=ALU.add)
                 if g == order[-1]:
@@ -502,26 +514,10 @@ def tile_model_pa_t_kernel(tc, en1, eps, W2, b2, Wm, Wv, gm, betam, gv, betav, o
             if g != order[-1]:
                 nc.sync.dma_start(out=out_chunks[g], in_=z[:])
 
-        a, b = order[0:2]
-        deviation(a)
-        deviation(b)
-        mean(a)
-        mean(b)
-        turn_deviation(a, 1)
-        turn_deviation(b, 1)
-        turn_mean(a)
-        turn_mean(b)
-        multiply(a)
-        multiply(b)
-        add_and_store(a)
-        add_and_store(b)
-        for i, g in enumerate(order):
-            if i in again:
-                second_products(again[i], "acc")
-            if i >= 2:
-                deviation(g)
-                mean(g)
-                turn_deviation(g, 1)
-                turn_mean(g)
-                multiply(g)
-                add_and_store(g)
+        pair = order[0:2]
+        for step in (deviation, mean, turn_deviation, turn_mean, multiply, add_and_store):
+            for g in pair:
+                step(g)
+        for g in order[2:]:
+            for step in (deviation, mean, turn_deviation, turn_mean, multiply, add_and_store):
+                step(g)

@@ -27,6 +27,7 @@ SPINS_AT_START = 5
 SPINS_AT_NORM = 4
 RAW_BUFS = 3
 LAST = CHUNKS - 1
+EARLY = LAST - 1
 KEPT = 2
 MEAN, VAR = 0, 1
 
@@ -50,7 +51,7 @@ def tile_model_pa_t_kernel(tc, en1, eps, W2, b2, Wm, Wv, gm, betam, gv, betav, o
         en2_pool = ctx.enter_context(tc.tile_pool(name="en2", bufs=FIRST_BATCH + 3))
         en2_codes_pool = ctx.enter_context(tc.tile_pool(name="en2codes", bufs=CHUNKS))
         z_pool = ctx.enter_context(tc.tile_pool(name="z", bufs=6))
-        stash_pool = ctx.enter_context(tc.tile_pool(name="stash", bufs=FIRST_BATCH))
+        stash_pool = ctx.enter_context(tc.tile_pool(name="stash", bufs=FIRST_BATCH + 1))
         tail_pool = ctx.enter_context(tc.tile_pool(name="tail", bufs=3))
         psum = ctx.enter_context(tc.psum_pool(name="psum", bufs=4))
 
@@ -75,10 +76,6 @@ def tile_model_pa_t_kernel(tc, en1, eps, W2, b2, Wm, Wv, gm, betam, gv, betav, o
         betav_raw = keep.tile([P, 1], BF16)
         with nc.allow_non_contiguous_dma(reason="128 short pieces, once"):
             nc.scalar.dma_start(out=b2_raw[:], in_=b2.rearrange("(p m) -> p m", m=PACK))
-            nc.scalar.dma_start(out=gm_raw[:], in_=gm.rearrange("(p o) -> p o", o=1))
-            nc.scalar.dma_start(out=gv_raw[:], in_=gv.rearrange("(p o) -> p o", o=1))
-            nc.scalar.dma_start(out=betam_raw[:], in_=betam.rearrange("(p o) -> p o", o=1))
-            nc.scalar.dma_start(out=betav_raw[:], in_=betav.rearrange("(p o) -> p o", o=1))
 
         def load_chunk(g):
             for h in range(2):
@@ -93,6 +90,11 @@ def tile_model_pa_t_kernel(tc, en1, eps, W2, b2, Wm, Wv, gm, betam, gv, betav, o
             nc.sync.dma_start(out=w2_raw[m][:], in_=w2_slabs[m])
         for g in range(1, RAW_BUFS):
             load_chunk(g)
+        with nc.allow_non_contiguous_dma(reason="128 short pieces, once"):
+            nc.sync.dma_start(out=gm_raw[:], in_=gm.rearrange("(p o) -> p o", o=1))
+            nc.sync.dma_start(out=gv_raw[:], in_=gv.rearrange("(p o) -> p o", o=1))
+            nc.sync.dma_start(out=betam_raw[:], in_=betam.rearrange("(p o) -> p o", o=1))
+            nc.sync.dma_start(out=betav_raw[:], in_=betav.rearrange("(p o) -> p o", o=1))
 
         zeros = keep.tile([P, CHUNK], BF16)
         nc.vector.memset(zeros[:], 0.0)
@@ -155,17 +157,18 @@ def tile_model_pa_t_kernel(tc, en1, eps, W2, b2, Wm, Wv, gm, betam, gv, betav, o
             words = raw[(g, h)][:].bitcast(F32)
             for c in range(PASSES):
                 bank = psum.tile([P, CHUNK], F32, tag="bank")
+                banks[(g, c, h)] = bank
                 if c == 0:
                     spin(bank, spins)
-                for jj in range(2):
-                    for u in range(2):
-                        first = ROW_WORDS * jj + 2 * P * c + P * u
-                        nc.tensor.transpose(
-                            bank[:, HALF * u + P * jj : HALF * u + P * (jj + 1)],
-                            words[:, first : first + P],
-                            ident[:],
-                        )
-                banks[(g, c, h)] = bank
+            order = [(c, jj) for c in range(PASSES) for jj in range(2)]
+            for c, jj in order:
+                for u in range(2):
+                    first = ROW_WORDS * jj + 2 * P * c + P * u
+                    nc.tensor.transpose(
+                        banks[(g, c, h)][:, HALF * u + P * jj : HALF * u + P * (jj + 1)],
+                        words[:, first : first + P],
+                        ident[:],
+                    )
 
         def copy_bank(copy, g, c, h):
             bank_in = grouped_pool.tile([P, HALF * PACK], BF16, align_bytes=64, tag="grouped")
@@ -227,11 +230,10 @@ def tile_model_pa_t_kernel(tc, en1, eps, W2, b2, Wm, Wv, gm, betam, gv, betav, o
                 expo[g] = e
             nc.scalar.activation(out=expo[g][:, m, :], in_=acc[:], func=ACT.Exp, bias=b2_f32[:, m : m + 1])
 
-        def logarithm(g, half=None):
-            if half in (None, 0):
+        def logarithm(g, cols=slice(0, CHUNK)):
+            if cols.start == 0:
                 soft = en2_pool.tile([P, CHUNK * PACK], BF16, align_bytes=64)
                 en2[g] = soft
-            cols = slice(0, CHUNK) if half is None else slice(HALF * half, HALF * (half + 1))
             nc.scalar.activation(
                 out=en2[g][:, PACK * cols.start : PACK * cols.stop].rearrange("p (q i t) -> p q t i", i=4, t=PACK),
                 in_=expo[g][:, :, cols].rearrange("p t (q i) -> p q t i", i=4),
@@ -271,13 +273,12 @@ def tile_model_pa_t_kernel(tc, en1, eps, W2, b2, Wm, Wv, gm, betam, gv, betav, o
         en2_codes = {}
         en2_scales = {}
 
-        def quantise_en2(g, half=None):
-            if half in (None, 0):
+        def quantise_en2(g, cols=slice(0, CHUNK)):
+            if cols.start == 0:
                 soft_codes = en2_codes_pool.tile([P, CHUNK], U32, align_bytes=64)
                 soft_scales = en2_codes_pool.tile([P, CHUNK], U8, align_bytes=64)
                 en2_codes[g] = soft_codes
                 en2_scales[g] = soft_scales
-            cols = slice(0, CHUNK) if half is None else slice(HALF * half, HALF * (half + 1))
             nc.vector.quantize_mx(
                 out=en2_codes[g][:, cols].bitcast(FP8X4),
                 scales=en2_scales[g][:, cols],
@@ -303,26 +304,48 @@ def tile_model_pa_t_kernel(tc, en1, eps, W2, b2, Wm, Wv, gm, betam, gv, betav, o
             second_product(g, MEAN, bank_m[:], slice(0, CHUNK))
             heads[g] = (bank_m[:], bank_v[:])
 
-        def second_products_of_half(g, half):
-            bank = psum.tile([P, CHUNK], F32, tag="bank")
-            cols = slice(HALF * half, HALF * (half + 1))
-            second_product(g, VAR, bank[:, HALF:CHUNK], cols)
-            second_product(g, MEAN, bank[:, 0:HALF], cols)
+        def second_products_of_half(g, half, bank, first, last):
+            cols = slice(HALF * half + first, HALF * half + last)
+            second_product(g, VAR, bank[:, HALF + first : HALF + last], cols)
+            second_product(g, MEAN, bank[:, first:last], cols)
             heads[(g, half)] = (bank[:, 0:HALF], bank[:, HALF:CHUNK])
 
-        stats = keep.tile([P, 2, CHUNKS + 1, 6], F32)
+        stats = keep.tile([P, 2, EARLY, 6], F32)
+        early = keep.tile([P, 2, 2], F32)
+        late = keep.tile([P, 2, 3 + 6 * (CHUNKS + 1 - EARLY)], F32)
+        nc.vector.memset(late[:, :, 0:1], 1.0 * EARLY * CHUNK)
 
         def statistics(piece, branch, entry):
-            nc.vector.bn_stats(out=stats[:, branch, entry, :], in_=heads[piece][branch])
+            if entry < EARLY:
+                place = stats[:, branch, entry, :]
+            else:
+                first = 3 + 6 * (entry - EARLY)
+                place = late[:, branch, first : first + 6]
+            nc.vector.bn_stats(out=place, in_=heads[piece][branch])
+
+        def gather_early():
+            for branch in (VAR, MEAN):
+                nc.vector.bn_aggr(
+                    out=early[:, branch, :], in_=stats[:, branch, :, :].rearrange("p g s -> p (g s)")
+                )
+            nc.vector.tensor_copy(out=late[:, :, 1:2], in_=early[:, :, 0:1])
+            nc.vector.tensor_scalar(
+                out=late[:, :, 2:3],
+                in0=early[:, :, 1:2],
+                scalar1=1.0 * EARLY * CHUNK,
+                scalar2=ROWS * BN_EPS,
+                op0=ALU.mult,
+                op1=ALU.add,
+            )
 
         def statistics_of_chunk(g):
             statistics(g, VAR, g)
             statistics(g, MEAN, g)
 
-        def stash(g):
+        def stash(g, copy=nc.vector.tensor_copy):
             kept = stash_pool.tile([P, 2, CHUNK], F32)
             for branch in range(2):
-                nc.vector.tensor_copy(out=kept[:, branch, :], in_=heads[g][branch])
+                copy(out=kept[:, branch, :], in_=heads[g][branch])
             heads[g] = (kept[:, MEAN, :], kept[:, VAR, :])
 
 
@@ -379,35 +402,38 @@ def tile_model_pa_t_kernel(tc, en1, eps, W2, b2, Wm, Wv, gm, betam, gv, betav, o
             if g == FIRST_BATCH:
                 stash(g - 1)
         statistics(LAST - 2, VAR, LAST - 2)
-        logarithm(LAST, 0)
-        quantise_en2(LAST, 0)
-        second_products_of_half(LAST, 0)
+        bank = psum.tile([P, CHUNK], F32, tag="bank")
+        logarithm(LAST, slice(0, HALF))
+        quantise_en2(LAST, slice(0, HALF))
+        second_products_of_half(LAST, 0, bank, 0, HALF)
         statistics(LAST - 2, MEAN, LAST - 2)
-        logarithm(LAST, 1)
-        quantise_en2(LAST, 1)
-        second_products_of_half(LAST, 1)
+        gather_early()
+        bank = psum.tile([P, CHUNK], F32, tag="bank")
+        for first in (0, P):
+            cols = slice(HALF + first, HALF + first + P)
+            logarithm(LAST, cols)
+            quantise_en2(LAST, cols)
+            second_products_of_half(LAST, 1, bank, first, first + P)
         statistics(LAST - 1, VAR, LAST - 1)
         statistics((LAST, 0), VAR, LAST)
         first_dev_bank = psum.tile([P, CHUNK], F32, tag="bank")
         spin(first_dev_bank, 2)
+        stash(5, nc.scalar.copy)
         nc.scalar.activation(out=warm[:], in_=one[:], func=ACT.Exp)
+        second_products(3, "acc")
 
         moments = keep.tile([P, 2, 2], F32)
-        spread = keep.tile([P, 2], F32)
         rstd = keep.tile([P, 2], F32)
         centre = keep.tile([P, 2], F32)
         scale = keep.tile([P, 2], F32)
         offset = keep.tile([P, 2], F32)
 
         def aggregate(branch):
-            nc.vector.bn_aggr(out=moments[:, branch, :], in_=stats[:, branch, :, :].rearrange("p g s -> p (g s)"))
+            nc.vector.bn_aggr(out=moments[:, branch, :], in_=late[:, branch, :])
 
         def power(branch):
             col = slice(branch, branch + 1)
-            nc.vector.tensor_scalar(
-                out=spread[:, col], in0=moments[:, branch, 1:2], scalar1=1.0, scalar2=BN_EPS, op0=ALU.mult, op1=ALU.add
-            )
-            nc.gpsimd.tensor_tensor(out=rstd[:, col], in0=spread[:, col], in1=neg_half[:, col], op=ALU.pow)
+            nc.gpsimd.tensor_tensor(out=rstd[:, col], in0=moments[:, branch, 1:2], in1=neg_half[:, col], op=ALU.pow)
 
         def scale_and_offset(branch):
             col = slice(branch, branch + 1)
@@ -428,20 +454,20 @@ def tile_model_pa_t_kernel(tc, en1, eps, W2, b2, Wm, Wv, gm, betam, gv, betav, o
         statistics((LAST, 1), VAR, LAST + 1)
         statistics((LAST, 0), MEAN, LAST)
         aggregate(VAR)
-        statistics((LAST, 1), MEAN, LAST + 1)
         power(VAR)
         nc.vector.memset(zeros[:, 0:2], 0.0)
         spin(first_dev_bank, 3)
+        statistics((LAST, 1), MEAN, LAST + 1)
         centre_of(VAR)
         statistics(LAST - 1, MEAN, LAST - 1)
-        aggregate(MEAN)
         scale_and_offset(VAR)
+        aggregate(MEAN)
         power(MEAN)
         centre_of(MEAN)
         scale_and_offset(MEAN)
 
-        order = [7, 5, 6, 0, 3, 1, 4, 2]
-        again = {5: 3, 0: 4}
+        order = [7, 6, 5, 0, 3, 1, 4, 2]
+        again = {6: 4}
         devs = {}
         means = {}
         dev_banks = {}

@@ -501,6 +501,7 @@ def tile_model_pa_t_kernel(tc, en1, eps, W2, b2, Wm, Wv, gm, betam, gv, betav, o
             bank = first_dev_bank
             if g != LAST:
                 bank = psum.tile([P, CHUNK], F32, tag="bank")
+                spin(bank, 1)
             turn(devs[g], bank)
             dev_banks[g] = bank
             if g in again:

@@ -202,7 +202,7 @@ def tile_model_pa_t_kernel(tc, en1, eps, W2, b2, Wm, Wv, gm, betam, gv, betav, o
             for c in range(PASSES):
                 quantise_bank(g, c, h)
 
-        transpose_slab(0, 5)
+        transpose_slab(0, 3)
         copy_slab(0)
         quantise_slab(0)
         front(0, 0, spins=1)
@@ -526,25 +526,17 @@ def tile_model_pa_t_kernel(tc, en1, eps, W2, b2, Wm, Wv, gm, betam, gv, betav, o
 
         def multiply(g):
             noise = tail_pool.tile([P, CHUNK], F32)
-            for cols in halves:
-                nc.vector.tensor_tensor(
-                    out=noise[:, cols], in0=dev_banks[g][:, cols], in1=hp["eps"][:, g, cols], op=ALU.mult
-                )
+            nc.vector.tensor_tensor(out=noise[:], in0=dev_banks[g][:], in1=hp["eps"][:, g, :], op=ALU.mult)
             noises[g] = noise
 
         def add_and_store(g):
             z = z_pool.tile([P, CHUNK], F32)
-            for cols in halves:
+            for cols in halves if g == order[-1] else (slice(0, CHUNK),):
                 nc.vector.tensor_tensor(out=z[:, cols], in0=mean_banks[g][:, cols], in1=noises[g][:, cols], op=ALU.add)
-                if g == order[-1]:
-                    nc.sync.dma_start(out=out_chunks[g][:, cols], in_=z[:, cols])
-            if g != order[-1]:
-                nc.sync.dma_start(out=out_chunks[g], in_=z[:])
+                nc.sync.dma_start(out=out_chunks[g][:, cols], in_=z[:, cols])
 
-        pair = order[0:2]
-        for step in (deviation, mean, turn_deviation, turn_mean, multiply, add_and_store):
-            for g in pair:
-                step(g)
-        for g in order[2:]:
+        for first in range(0, CHUNKS, 2):
+            pair = order[first : first + 2]
             for step in (deviation, mean, turn_deviation, turn_mean, multiply, add_and_store):
-                step(g)
+                for g in pair:
+                    step(g)

@@ -196,7 +196,7 @@ def tile_model_pa_t_kernel(tc, en1, eps, W2, b2, Wm, Wv, gm, betam, gv, betav, o
             if h == 1 and g + RAW_BUFS < CHUNKS:
                 load_chunk(g + RAW_BUFS)
             for c in range(PASSES):
-                copy_bank(nc.scalar.copy if c == 1 and g < FIRST_BATCH else nc.vector.tensor_copy, g, c, h)
+                copy_bank(nc.scalar.copy if c == 1 and g <= FIRST_BATCH and (g, h) != (FIRST_BATCH, 1) else nc.vector.tensor_copy, g, c, h)
             if h == 0:
                 open_codes(g)
             for c in range(PASSES):
@@ -364,22 +364,26 @@ def tile_model_pa_t_kernel(tc, en1, eps, W2, b2, Wm, Wv, gm, betam, gv, betav, o
             bank_of_product(0, m)
         front_of_chunk(2)
         banks_of_chunk(1)
+        front(3, 0)
         banks_of_chunk(2)
         for g in range(FIRST_BATCH):
             logarithm(g)
-        front_of_chunk(3)
+        front(3, 1)
         front_of_chunk(4)
+        front_of_chunk(5)
         bank_of_product(3, 0)
         bank_of_product(3, 1)
-        front(5, 0)
+        front(6, 0)
         bank_of_product(3, 2)
-        front(5, 1)
         bank_of_product(3, 3)
-        for g, h in ((6, 0), (6, 1), (7, 0)):
-            front(g, h, spins=2)
-        banks_of_chunk(4)
+        front(6, 1, spins=1)
+        front(7, 0, spins=2)
+        bank_of_product(4, 0)
+        bank_of_product(4, 1)
         front(7, 1)
         head_prep()
+        bank_of_product(4, 2)
+        bank_of_product(4, 3)
         banks_of_chunk(5)
         banks_of_chunk(6)
         banks_of_chunk(7)

from contextlib import ExitStack

import concourse.mybir as mybir
from concourse.masks import make_identity

F32 = mybir.dt.float32
BF16 = mybir.dt.bfloat16
U32 = mybir.dt.uint32
U8 = mybir.dt.uint8
FP8X4 = mybir.dt.float8_e4m3fn_x4
ACT = mybir.ActivationFunctionType
ALU = mybir.AluOpType

P = 128
PACK = 4
ROWS, K1, HIDDEN, OUTS = 4096, 1024, 512, 128
CHUNK = 512
CHUNKS = ROWS // CHUNK
SUB = CHUNK // P
PASSES = K1 // (P * PACK)
HALF = CHUNK // 2
ROW_WORDS = K1 // 2
BN_EPS = 1e-5

FIRST_BATCH = 3
SPINS_AT_START = 5
SPINS_AT_NORM = 4
RAW_BUFS = 3
LAST = CHUNKS - 1
EARLY = LAST - 1
KEPT = 2
MEAN, VAR = 0, 1

FLOPS = 2 * ROWS * K1 * HIDDEN + 2 * 2 * ROWS * HIDDEN * OUTS


def tile_model_pa_t_kernel(tc, en1, eps, W2, b2, Wm, Wv, gm, betam, gv, betav, out):
    nc = tc.nc
    en1_halves = en1.rearrange("(g p h j) k -> g h p (j k)", p=P, h=2, j=2)
    w2_slabs = W2.rearrange("(p m) k -> m p k", m=PACK)
    eps_chunks = eps.rearrange("(g p j) c -> p g (j c)", p=P, j=SUB)
    out_chunks = out.rearrange("(g p j) c -> g p (j c)", p=P, j=SUB)

    with ExitStack() as ctx:
        ctx.enter_context(tc.manual_schedule())
        keep = ctx.enter_context(tc.tile_pool(name="keep", bufs=1))
        raw_pool = ctx.enter_context(tc.tile_pool(name="raw", bufs=2 * RAW_BUFS))
        grouped_pool = ctx.enter_context(tc.tile_pool(name="grouped", bufs=8))
        codes_pool = ctx.enter_context(tc.tile_pool(name="codes", bufs=6))
        exp_pool = ctx.enter_context(tc.tile_pool(name="exp", bufs=max(FIRST_BATCH, CHUNKS - FIRST_BATCH)))
        en2_pool = ctx.enter_context(tc.tile_pool(name="en2", bufs=FIRST_BATCH + 3))
        en2_codes_pool = ctx.enter_context(tc.tile_pool(name="en2codes", bufs=CHUNKS))
        z_pool = ctx.enter_context(tc.tile_pool(name="z", bufs=6))
        stash_pool = ctx.enter_context(tc.tile_pool(name="stash", bufs=FIRST_BATCH + 1))
        tail_pool = ctx.enter_context(tc.tile_pool(name="tail", bufs=3))
        psum = ctx.enter_context(tc.psum_pool(name="psum", bufs=4))

        raw = {}
        banks = {}
        grouped = {}
        codes = {}
        scales = {}
        w2_banks = {}
        w2_grouped = {}
        w2_codes = {}
        w2_scales = {}
        sums = {}
        expo = {}
        en2 = {}
        heads = {}

        b2_raw = keep.tile([P, PACK], BF16)
        gm_raw = keep.tile([P, 1], BF16)
        gv_raw = keep.tile([P, 1], BF16)
        betam_raw = keep.tile([P, 1], BF16)
        betav_raw = keep.tile([P, 1], BF16)
        with nc.allow_non_contiguous_dma(reason="128 short pieces, once"):
            nc.scalar.dma_start(out=b2_raw[:], in_=b2.rearrange("(p m) -> p m", m=PACK))

        def load_chunk(g):
            for h in range(2):
                x_raw = raw_pool.tile([P, 2 * K1], BF16)
                nc.sync.dma_start(out=x_raw[:], in_=en1_halves[g, h])
                raw[(g, h)] = x_raw

        w2_raw = [keep.tile([P, K1], BF16, tag="w2_raw%d" % m, name="w2_raw%d" % m) for m in range(PACK)]
        nc.sync.dma_start(out=w2_raw[0][:], in_=w2_slabs[0])
        load_chunk(0)
        for m in range(1, PACK):
            nc.sync.dma_start(out=w2_raw[m][:], in_=w2_slabs[m])
        for g in range(1, RAW_BUFS):
            load_chunk(g)
        with nc.allow_non_contiguous_dma(reason="128 short pieces, once"):
            nc.sync.dma_start(out=gm_raw[:], in_=gm.rearrange("(p o) -> p o", o=1))
            nc.sync.dma_start(out=gv_raw[:], in_=gv.rearrange("(p o) -> p o", o=1))
            nc.sync.dma_start(out=betam_raw[:], in_=betam.rearrange("(p o) -> p o", o=1))
            nc.sync.dma_start(out=betav_raw[:], in_=betav.rearrange("(p o) -> p o", o=1))

        zeros = keep.tile([P, CHUNK], BF16)
        nc.vector.memset(zeros[:], 0.0)

        def spin(bank, count):
            for i in range(count):
                nc.tensor.matmul(out=bank[:], lhsT=zeros[:, 0:P], rhs=zeros[:], start=True, stop=True)


        one = keep.tile([P, 1], F32)
        nc.vector.memset(one[:], 1.0)
        warm = keep.tile([P, 1], F32)
        nc.scalar.activation(out=warm[:], in_=one[:], func=ACT.Exp)

        ident = keep.tile([P, P], F32)
        make_identity(nc, ident[:])
        neg_half = keep.tile([P, 2], F32)
        nc.gpsimd.memset(neg_half[:], -0.5)
        b2_f32 = keep.tile([P, PACK], F32)
        nc.gpsimd.tensor_copy(out=b2_f32[:], in_=b2_raw[:])
        gain = keep.tile([P, 2], F32)
        neg_gain = keep.tile([P, 2], F32)
        shift = keep.tile([P, 2], F32)
        nc.gpsimd.tensor_copy(out=gain[:, 0:1], in_=gm_raw[:])
        nc.gpsimd.tensor_scalar(out=gain[:, 1:2], in0=gv_raw[:], scalar1=0.5, scalar2=0.0, op0=ALU.mult, op1=ALU.add)
        nc.gpsimd.tensor_scalar(out=neg_gain[:], in0=gain[:], scalar1=-1.0, scalar2=0.0, op0=ALU.mult, op1=ALU.add)
        nc.gpsimd.tensor_copy(out=shift[:, 0:1], in_=betam_raw[:])
        nc.gpsimd.tensor_scalar(out=shift[:, 1:2], in0=betav_raw[:], scalar1=0.5, scalar2=0.0, op0=ALU.mult, op1=ALU.add)

        def transpose_slab(m, spins=0):
            words = w2_raw[m][:].bitcast(F32)
            bank = psum.tile([P, CHUNK], F32, tag="bank")
            spin(bank, spins)
            for plane in range(2 * PASSES):
                nc.tensor.transpose(
                    bank[:, P * plane : P * (plane + 1)], words[:, P * plane : P * (plane + 1)], ident[:]
                )
            w2_banks[m] = bank

        def copy_slab(m):
            slab_in = grouped_pool.tile([P, HALF * PACK], BF16, align_bytes=64, tag="grouped")
            nc.scalar.copy(
                out=slab_in[:].bitcast(F32).rearrange("p (c r u) -> p c r u", c=PASSES, u=2),
                in_=w2_banks[m][:].rearrange("p (c u r) -> p c r u", c=PASSES, u=2),
            )
            w2_grouped[m] = slab_in

        def quantise_slab(m):
            slab_codes = keep.tile([P, PASSES, P], U32, align_bytes=64, tag="w2_codes%d" % m)
            slab_scales = keep.tile([P, PASSES, P], U8, align_bytes=64, tag="w2_scales%d" % m)
            nc.vector.quantize_mx(
                out=slab_codes[:].rearrange("p c r -> p (c r)").bitcast(FP8X4),
                scales=slab_scales[:].rearrange("p c r -> p (c r)"),
                in_=w2_grouped[m][:],
            )
            w2_codes[m] = slab_codes
            w2_scales[m] = slab_scales

        def transpose_half(g, h, spins):
            words = raw[(g, h)][:].bitcast(F32)
            for c in range(PASSES):
                bank = psum.tile([P, CHUNK], F32, tag="bank")
                banks[(g, c, h)] = bank
                if c == 0:
                    spin(bank, spins)
            order = [(c, jj) for c in range(PASSES) for jj in range(2)]
            for c, jj in order:
                for u in range(2):
                    first = ROW_WORDS * jj + 2 * P * c + P * u
                    nc.tensor.transpose(
                        banks[(g, c, h)][:, HALF * u + P * jj : HALF * u + P * (jj + 1)],
                        words[:, first : first + P],
                        ident[:],
                    )

        def copy_bank(copy, g, c, h):
            bank_in = grouped_pool.tile([P, HALF * PACK], BF16, align_bytes=64, tag="grouped")
            copy(
                out=bank_in[:].bitcast(F32).rearrange("p (r u) -> p r u", u=2),
                in_=banks[(g, c, h)][:].rearrange("p (u r) -> p r u", u=2),
            )
            grouped[(g, c, h)] = bank_in

        def open_codes(g):
            chunk_codes = codes_pool.tile([P, PASSES, CHUNK], U32, align_bytes=64)
            chunk_scales = codes_pool.tile([P, PASSES, CHUNK], U8, align_bytes=64)
            codes[g] = chunk_codes
            scales[g] = chunk_scales

        def quantise_bank(g, c, h):
            nc.vector.quantize_mx(
                out=codes[g][:, c, HALF * h : HALF * (h + 1)].bitcast(FP8X4),
                scales=scales[g][:, c, HALF * h : HALF * (h + 1)],
                in_=grouped[(g, c, h)][:],
            )

        def front(g, h, spins=0):
            transpose_half(g, h, spins)
            if h == 1 and g + RAW_BUFS < CHUNKS:
                load_chunk(g + RAW_BUFS)
            for c in range(PASSES):
                copy_bank(nc.scalar.copy if c == 1 and g <= FIRST_BATCH and (g, h) != (FIRST_BATCH, 1) else nc.vector.tensor_copy, g, c, h)
            if h == 0:
                open_codes(g)
            for c in range(PASSES):
                quantise_bank(g, c, h)

        transpose_slab(0, 3)
        copy_slab(0)
        quantise_slab(0)
        front(0, 0, spins=1)
        front(0, 1, spins=1)
        for m in range(1, PACK):
            transpose_slab(m, spins=(0, 1, 0, 0)[m])
            copy_slab(m)
        for m in range(1, PACK):
            quantise_slab(m)

        def bank_of_product(g, m):
            acc = psum.tile([P, CHUNK], F32, tag="acc")
            for c in range(PASSES):
                nc.tensor.matmul_mx(
                    out=acc[:],
                    lhsT=w2_codes[m][:, c, :].bitcast(FP8X4),
                    lhsT_scale=w2_scales[m][:, c, :],
                    rhs=codes[g][:, c, :].bitcast(FP8X4),
                    rhs_scale=scales[g][:, c, :],
                    start=(c == 0),
                    stop=(c == PASSES - 1),
                )
            if m == 0:
                e = exp_pool.tile([P, PACK, CHUNK], F32)
                expo[g] = e
            nc.scalar.activation(out=expo[g][:, m, :], in_=acc[:], func=ACT.Exp, bias=b2_f32[:, m : m + 1])

        def logarithm(g, cols=slice(0, CHUNK)):
            if cols.start == 0:
                soft = en2_pool.tile([P, CHUNK * PACK], BF16, align_bytes=64)
                en2[g] = soft
            nc.scalar.activation(
                out=en2[g][:, PACK * cols.start : PACK * cols.stop].rearrange("p (q i t) -> p q t i", i=4, t=PACK),
                in_=expo[g][:, :, cols].rearrange("p t (q i) -> p q t i", i=4),
                func=ACT.Ln,
                bias=one[:],
            )

        hp = {}
        def head_prep():
            wm_raw = keep.tile([P, HIDDEN], BF16)
            nc.sync.dma_start(out=wm_raw[:], in_=Wm)
            wv_raw = keep.tile([P, HIDDEN], BF16)
            nc.sync.dma_start(out=wv_raw[:], in_=Wv)
            eps_rows = keep.tile([P, CHUNKS, CHUNK], BF16)
            nc.sync.dma_start(out=eps_rows[:], in_=eps_chunks)

            head_bank = psum.tile([P, CHUNK], F32, tag="bank")
            for branch, head_raw in enumerate((wm_raw, wv_raw)):
                planes = head_raw[:].bitcast(F32).rearrange("p (q u) -> p u q", u=2)
                for u in range(2):
                    nc.tensor.transpose(
                        head_bank[:, HALF * u + P * branch : HALF * u + P * (branch + 1)], planes[:, u, :], ident[:]
                    )
            head_grouped = keep.tile([P, 2 * OUTS * PACK], BF16, align_bytes=64)
            nc.vector.tensor_copy(
                out=head_grouped[:].bitcast(F32).rearrange("p (r u) -> p r u", u=2),
                in_=head_bank[:].rearrange("p (u r) -> p r u", u=2),
            )
            head_codes = keep.tile([P, 2 * OUTS], U32, align_bytes=64)
            head_scales = keep.tile([P, 2 * OUTS], U8, align_bytes=64)
            nc.vector.quantize_mx(out=head_codes[:].bitcast(FP8X4), scales=head_scales[:], in_=head_grouped[:])


            hp["eps"] = eps_rows
            hp["codes"] = head_codes
            hp["scales"] = head_scales
        en2_codes = {}
        en2_scales = {}

        def quantise_en2(g, cols=slice(0, CHUNK)):
            if cols.start == 0:
                soft_codes = en2_codes_pool.tile([P, CHUNK], U32, align_bytes=64)
                soft_scales = en2_codes_pool.tile([P, CHUNK], U8, align_bytes=64)
                en2_codes[g] = soft_codes
                en2_scales[g] = soft_scales
            nc.vector.quantize_mx(
                out=en2_codes[g][:, cols].bitcast(FP8X4),
                scales=en2_scales[g][:, cols],
                in_=en2[g][:, PACK * cols.start : PACK * cols.stop],
            )

        def second_product(g, branch, head, cols):
            nc.tensor.matmul_mx(
                out=head,
                lhsT=hp["codes"][:, OUTS * branch : OUTS * (branch + 1)].bitcast(FP8X4),
                lhsT_scale=hp["scales"][:, OUTS * branch : OUTS * (branch + 1)],
                rhs=en2_codes[g][:, cols].bitcast(FP8X4),
                rhs_scale=en2_scales[g][:, cols],
                start=True,
                stop=True,
            )

        def second_products(g, tag, spins=0):
            bank_v = psum.tile([P, CHUNK], F32, tag=tag)
            spin(bank_v, spins)
            second_product(g, VAR, bank_v[:], slice(0, CHUNK))
            bank_m = psum.tile([P, CHUNK], F32, tag=tag)
            second_product(g, MEAN, bank_m[:], slice(0, CHUNK))
            heads[g] = (bank_m[:], bank_v[:])

        def second_products_of_half(g, half, bank, first, last):
            cols = slice(HALF * half + first, HALF * half + last)
            second_product(g, VAR, bank[:, HALF + first : HALF + last], cols)
            second_product(g, MEAN, bank[:, first:last], cols)
            heads[(g, half)] = (bank[:, 0:HALF], bank[:, HALF:CHUNK])

        stats = keep.tile([P, 2, EARLY, 6], F32)
        early = keep.tile([P, 2, 2], F32)
        late = keep.tile([P, 2, 3 + 6 * (CHUNKS + 1 - EARLY)], F32)
        nc.vector.memset(late[:, :, 0:1], 1.0 * EARLY * CHUNK)

        def statistics(piece, branch, entry):
            if entry < EARLY:
                place = stats[:, branch, entry, :]
            else:
                first = 3 + 6 * (entry - EARLY)
                place = late[:, branch, first : first + 6]
            nc.vector.bn_stats(out=place, in_=heads[piece][branch])

        def gather_early():
            for branch in (VAR, MEAN):
                nc.vector.bn_aggr(
                    out=early[:, branch, :], in_=stats[:, branch, :, :].rearrange("p g s -> p (g s)")
                )
            nc.vector.tensor_copy(out=late[:, :, 1:2], in_=early[:, :, 0:1])
            nc.vector.tensor_scalar(
                out=late[:, :, 2:3],
                in0=early[:, :, 1:2],
                scalar1=1.0 * EARLY * CHUNK,
                scalar2=ROWS * BN_EPS,
                op0=ALU.mult,
                op1=ALU.add,
            )

        def statistics_of_chunk(g):
            statistics(g, VAR, g)
            statistics(g, MEAN, g)

        def stash(g, copy=nc.vector.tensor_copy):
            kept = stash_pool.tile([P, 2, CHUNK], F32)
            for branch in range(2):
                copy(out=kept[:, branch, :], in_=heads[g][branch])
            heads[g] = (kept[:, MEAN, :], kept[:, VAR, :])


        def banks_of_chunk(g):
            for m in range(PACK):
                bank_of_product(g, m)

        def front_of_chunk(g):
            for h in range(2):
                front(g, h)

        for m in range(2):
            bank_of_product(0, m)
        front_of_chunk(1)
        for m in range(2, PACK):
            bank_of_product(0, m)
        front_of_chunk(2)
        banks_of_chunk(1)
        front(3, 0)
        banks_of_chunk(2)
        for g in range(FIRST_BATCH):
            logarithm(g)
        front(3, 1)
        front_of_chunk(4)
        front_of_chunk(5)
        bank_of_product(3, 0)
        bank_of_product(3, 1)
        front(6, 0)
        bank_of_product(3, 2)
        bank_of_product(3, 3)
        front(6, 1, spins=1)
        front(7, 0, spins=2)
        bank_of_product(4, 0)
        bank_of_product(4, 1)
        front(7, 1)
        head_prep()
        bank_of_product(4, 2)
        bank_of_product(4, 3)
        banks_of_chunk(5)
        banks_of_chunk(6)
        banks_of_chunk(7)

        for g in range(FIRST_BATCH):
            quantise_en2(g)
        for g in range(2):
            second_products(g, "bank")
        for g in range(2):
            statistics_of_chunk(g)
            stash(g)
            if g == 0:
                second_products(2, "bank")
        for g in range(FIRST_BATCH, LAST):
            logarithm(g)
            quantise_en2(g)
            second_products(g, "acc" if g >= LAST - KEPT else "bank", spins=1)
            if g < LAST - 1:
                statistics_of_chunk(g - 1)
            if g == FIRST_BATCH:
                stash(g - 1)
        statistics(LAST - 2, VAR, LAST - 2)
        bank = psum.tile([P, CHUNK], F32, tag="bank")
        logarithm(LAST, slice(0, HALF))
        quantise_en2(LAST, slice(0, HALF))
        second_products_of_half(LAST, 0, bank, 0, HALF)
        statistics(LAST - 2, MEAN, LAST - 2)
        gather_early()
        bank = psum.tile([P, CHUNK], F32, tag="bank")
        for first in (0, P):
            cols = slice(HALF + first, HALF + first + P)
            logarithm(LAST, cols)
            quantise_en2(LAST, cols)
            second_products_of_half(LAST, 1, bank, first, first + P)
        statistics(LAST - 1, VAR, LAST - 1)
        statistics((LAST, 0), VAR, LAST)
        first_dev_bank = psum.tile([P, CHUNK], F32, tag="bank")
        spin(first_dev_bank, 2)
        stash(5, nc.scalar.copy)
        nc.scalar.activation(out=warm[:], in_=one[:], func=ACT.Exp)
        second_products(3, "acc")

        moments = keep.tile([P, 2, 2], F32)
        rstd = keep.tile([P, 2], F32)
        centre = keep.tile([P, 2], F32)
        scale = keep.tile([P, 2], F32)
        offset = keep.tile([P, 2], F32)

        def aggregate(branch):
            nc.vector.bn_aggr(out=moments[:, branch, :], in_=late[:, branch, :])

        def power(branch):
            col = slice(branch, branch + 1)
            nc.gpsimd.tensor_tensor(out=rstd[:, col], in0=moments[:, branch, 1:2], in1=neg_half[:, col], op=ALU.pow)

        def scale_and_offset(branch):
            col = slice(branch, branch + 1)
            nc.vector.tensor_tensor(out=scale[:, col], in0=rstd[:, col], in1=gain[:, col], op=ALU.mult)
            nc.vector.scalar_tensor_tensor(
                out=offset[:, col],
                in0=centre[:, col],
                scalar=rstd[:, col],
                in1=shift[:, col],
                op0=ALU.mult,
                op1=ALU.add,
            )

        def centre_of(branch):
            col = slice(branch, branch + 1)
            nc.vector.tensor_tensor(out=centre[:, col], in0=moments[:, branch, 0:1], in1=neg_gain[:, col], op=ALU.mult)

        statistics((LAST, 1), VAR, LAST + 1)
        statistics((LAST, 0), MEAN, LAST)
        aggregate(VAR)
        power(VAR)
        nc.vector.memset(zeros[:, 0:2], 0.0)
        spin(first_dev_bank, 3)
        statistics((LAST, 1), MEAN, LAST + 1)
        centre_of(VAR)
        statistics(LAST - 1, MEAN, LAST - 1)
        scale_and_offset(VAR)
        aggregate(MEAN)
        power(MEAN)
        centre_of(MEAN)
        scale_and_offset(MEAN)

        order = [7, 6, 5, 0, 3, 1, 4, 2]
        again = {6: 4}
        devs = {}
        means = {}
        dev_banks = {}
        mean_banks = {}
        noises = {}

        def parts_of(g, branch):
            if g == LAST:
                return [(heads[(LAST, half)][branch], slice(HALF * half, HALF * (half + 1))) for half in range(2)]
            return [(heads[g][branch], slice(0, CHUNK))]

        def deviation(g):
            dev_t = tail_pool.tile([P, CHUNK], F32)
            for head, cols in parts_of(g, VAR):
                nc.scalar.activation(out=dev_t[:, cols], in_=head, func=ACT.Exp, scale=scale[:, 1:2], bias=offset[:, 1:2])
            devs[g] = dev_t

        def mean(g):
            mean_t = tail_pool.tile([P, CHUNK], F32)
            for head, cols in parts_of(g, MEAN):
                nc.scalar.activation(
                    out=mean_t[:, cols], in_=head, func=ACT.Identity, scale=scale[:, 0:1], bias=offset[:, 0:1]
                )
            means[g] = mean_t

        def turn(source, bank):
            for j in range(SUB):
                nc.tensor.transpose(bank[:, P * j : P * (j + 1)], source[:, P * j : P * (j + 1)], ident[:])

        def turn_deviation(g):
            bank = first_dev_bank
            if g != LAST:
                bank = psum.tile([P, CHUNK], F32, tag="bank")
                spin(bank, 1)
            turn(devs[g], bank)
            dev_banks[g] = bank
            if g in again:
                again_product(again[g], VAR)

        def turn_mean(g):
            bank = psum.tile([P, CHUNK], F32, tag="bank")
            turn(means[g], bank)
            mean_banks[g] = bank
            if g in again:
                again_product(again[g], MEAN)

        def again_product(g, branch):
            bank = psum.tile([P, CHUNK], F32, tag="acc")
            second_product(g, branch, bank[:], slice(0, CHUNK))
            if branch == VAR:
                heads[g] = (None, bank[:])
            else:
                heads[g] = (bank[:], heads[g][VAR])

        halves = (slice(0, HALF), slice(HALF, CHUNK))

        def multiply(g):
            noise = tail_pool.tile([P, CHUNK], F32)
            nc.vector.tensor_tensor(out=noise[:], in0=dev_banks[g][:], in1=hp["eps"][:, g, :], op=ALU.mult)
            noises[g] = noise

        def add_and_store(g):
            z = z_pool.tile([P, CHUNK], F32)
            for cols in halves if g == order[-1] else (slice(0, CHUNK),):
                nc.vector.tensor_tensor(out=z[:, cols], in0=mean_banks[g][:, cols], in1=noises[g][:, cols], op=ALU.add)
                nc.sync.dma_start(out=out_chunks[g][:, cols], in_=z[:, cols])

        for first in range(0, CHUNKS, 2):
            pair = order[first : first + 2]
            for step in (deviation, mean, turn_deviation, turn_mean, multiply, add_and_store):
                for g in pair:
                    step(g)
